import numpy as np
import ml_dtypes


def mxq(x, axis, fmt="e4m3"):
    dtype, down = {"e4m3": (ml_dtypes.float8_e4m3fn, 7), "e5m2": (ml_dtypes.float8_e5m2, 14)}[fmt]
    v = np.moveaxis(np.asarray(x, np.float32).astype(ml_dtypes.bfloat16).astype(np.float64), axis, -1)
    blocks = v.reshape(v.shape[:-1] + (-1, 32))
    amax = np.abs(blocks).max(-1, keepdims=True)
    byte = np.maximum(np.where(amax > 0, np.frexp(amax)[1] - 1 + 127, 0) - down, 1)
    scale = np.exp2(byte - 127.0)
    codes = (blocks / scale).astype(np.float32).astype(dtype).astype(np.float64)
    return np.moveaxis((codes * scale).reshape(v.shape), -1, axis)


WIDE = False


def mx_kscale(k):
    if not WIDE:
        return np.ones(k)
    levels = np.array([10, -10, 5, -5, 0])
    a = np.random.permutation(np.resize(levels, k // 512 * 4)).reshape(k // 512, 4)
    idx = np.arange(k)
    return np.exp2(a[idx // 512, idx % 128 // 32])


BF16 = ml_dtypes.bfloat16


def bf(x):
    return np.asarray(x, np.float32).astype(BF16)


def f64(x):
    return np.asarray(x).astype(np.float64)


B, S, HID, H, D, CHUNK = 1, 2048, 1024, 8, 128, 512
NC = S // CHUNK
MASK_VALUE = -1e9


def setup_inputs():
    s = mx_kscale(HID)
    return {"q": bf(np.random.standard_normal((B, H, S, D)) * 1.4),
            "k_scaled": bf(np.random.standard_normal((B, H, S, D)) * 1.4 / np.sqrt(D)),
            "hidden_states": bf(np.random.standard_normal((B, S, HID)) * s),
            "Wv": bf(np.random.standard_normal((HID, H * D)) / np.sqrt(HID) / s[:, None])}


def reference(q, k_scaled, hidden_states, Wv):
    q, k = f64(q), f64(k_scaled)
    v = mxq(f64(hidden_states), 2, "e4m3") @ mxq(f64(Wv), 0, "e4m3")
    v = v.reshape(B, S, H, D).transpose(0, 2, 1, 3)
    vq = mxq(v, 2, "e4m3")
    pos = np.arange(S)
    outs = []
    for n in range(NC):
        lo, mid, hi = max(n - 1, 0) * CHUNK, n * CHUNK, (n + 1) * CHUNK
        dots = q[:, :, mid:hi] @ k[:, :, lo:hi].transpose(0, 1, 3, 2)
        causal = pos[mid:hi, None] >= pos[None, lo:hi]
        dots = np.where(causal, dots, MASK_VALUE)
        e = np.exp(dots - dots.max(-1, keepdims=True))
        outs.append((mxq(e, 3, "e4m3") @ vq[:, :, lo:hi]) / e.sum(-1, keepdims=True))
    out = np.concatenate(outs, axis=2)
    return out.transpose(0, 2, 1, 3).reshape(B, S, H * D)

@@ -1,0 +1,421 @@
+from contextlib import ExitStack
+
+import concourse.mybir as mybir
+from concourse.masks import make_identity
+
+F32 = mybir.dt.float32
+BF16 = mybir.dt.bfloat16
+U32 = mybir.dt.uint32
+U8 = mybir.dt.uint8
+FP8X4 = mybir.dt.float8_e4m3fn_x4
+ACT = mybir.ActivationFunctionType
+ALU = mybir.AluOpType
+AXIS_X = mybir.AxisListType.X
+
+P = 128
+S, HID, H, D, CHUNK = 2048, 1024, 8, 128, 512
+MASK_VALUE = -1e9
+K_PASS = 4 * P
+N_CHUNKS = S // CHUNK
+QT = CHUNK // P
+N_GROUPS = N_CHUNKS * H
+N_BLOCKS = N_GROUPS * QT
+HID_PASSES = HID // K_PASS
+
+LAG = 12
+V_BEHIND = LAG // QT - 1
+QK_AHEAD = 5
+
+FLOPS = 2 * S * HID * H * D + 2 * (2 * H * D * CHUNK * (CHUNK + (N_CHUNKS - 1) * 2 * CHUNK))
+
+
+def place(block):
+    group, t = divmod(block, QT)
+    chunk, head = divmod(group, H)
+    return group, chunk, head, t
+
+
+def hs_job(tick):
+    group, phase = divmod(tick, QT)
+    chunk, head = divmod(group, H)
+    if 0 <= chunk < N_CHUNKS and head < 2 and phase >= 2:
+        return chunk, 2 * head + phase - 2
+    return None
+
+
+def tile_localselfattention_pa_kernel(tc, q, k_scaled, hidden_states, Wv, out):
+    nc = tc.nc
+    q_rows = q.flatten_outer_dims()
+    k_rows = k_scaled.flatten_outer_dims()
+    hs_rows = hidden_states.flatten_outer_dims()
+    out_rows = out.flatten_outer_dims()
+
+    with ExitStack() as stack:
+        stack.enter_context(tc.manual_schedule())
+
+        def ring(name, depth):
+            return stack.enter_context(tc.tile_pool(name=name, bufs=depth))
+
+        fixed = ring("fixed", 1)
+        banks = stack.enter_context(tc.psum_pool(name="banks", bufs=1))
+
+        score_bank = [banks.tile([P, CHUNK], F32, name="score_bank%d" % n) for n in range(4)]
+        flip_bank = [banks.tile([P, 4, P], F32, name="flip_bank%d" % n) for n in range(2)]
+        out_bank = banks.tile([P, QT, D], F32, name="out_bank")
+        side_bank = banks.tile([P, 4 * P], F32, name="side_bank")
+        side_words = side_bank[:].rearrange("p (j r) -> p j r", r=P)
+        side_halves = side_bank[:].bitcast(BF16)
+
+        ident_f = fixed.tile([P, P], F32, name="ident_f")
+        ident_b = fixed.tile([P, P], BF16, name="ident_b")
+        mask_f = fixed.tile([P, P], F32, name="mask_f")
+        mask_b = fixed.tile([P, P], BF16, name="mask_b")
+        e_rows = [fixed.tile([P, 2 * CHUNK], BF16, name="e_rows%d" % t) for t in range(QT)]
+
+        wv_in = fixed.tile([P, HID_PASSES, 4, H * D], BF16, name="wv_in")
+        wv_codes = fixed.tile([P, H * HID_PASSES * D], U32, name="wv_codes", align_bytes=64)
+        wv_scales = fixed.tile([P, H * HID_PASSES * D], U8, name="wv_scales", align_bytes=64)
+        v_codes = [fixed.tile([P, H * D], U32, name="v_codes%d" % c, align_bytes=64) for c in range(N_CHUNKS)]
+        v_scales = [fixed.tile([P, H * D], U8, name="v_scales%d" % c, align_bytes=64) for c in range(N_CHUNKS)]
+
+        qk_in_ring = ring("qk_in", QK_AHEAD)
+        qk_t_ring = ring("qk_t", H + 2)
+        hs_in_ring = ring("hs_in", 2)
+        hs_grouped_ring = ring("hs_grouped", 2)
+        hs_mx_ring = ring("hs_mx", 2)
+        wv_grouped_ring = ring("wv_grouped", 2)
+        v_grouped_ring = ring("v_grouped", 2)
+        max_ring = ring("max", 3)
+        sum_ring = ring("sum", 3)
+        inverse_ring = ring("inverse", LAG // QT + 2)
+        e_grouped_ring = ring("e_grouped", 3)
+        e_mx_ring = ring("e_mx", LAG)
+        out_ring = ring("out", 3)
+
+        qk_in, qk_t, hs_in, hs_grouped, hs_codes, hs_scales = {}, {}, {}, {}, {}, {}
+        wv_grouped, v_grouped, top, neg_top, row_sum, total, inverse = {}, {}, {}, {}, {}, {}, {}
+        e_grouped, e_codes, e_scales, out_sb = {}, {}, {}, {}
+
+        def load_qk(group):
+            if not 0 <= group < N_GROUPS:
+                return
+            chunk, head = divmod(group, H)
+            rows = slice(head * S + chunk * CHUNK, head * S + (chunk + 1) * CHUNK)
+            qk_in[group] = qk_in_ring.tile([P, 2, QT, D], BF16, name="qk_in")
+            nc.sync.dma_start(out=qk_in[group][:, 0], in_=q_rows[rows, :].rearrange("(t p) d -> p t d", p=P))
+            nc.sync.dma_start(out=qk_in[group][:, 1], in_=k_rows[rows, :].rearrange("(t p) d -> p t d", p=P))
+
+        def load_hs(chunk):
+            if not 0 <= chunk < N_CHUNKS:
+                return
+            hs_in[chunk] = hs_in_ring.tile([P, 4, HID], BF16, name="hs_in")
+            nc.sync.dma_start(
+                out=hs_in[chunk][:].rearrange("p (u e) k -> p u e k", e=2),
+                in_=hs_rows[chunk * CHUNK : (chunk + 1) * CHUNK, :].rearrange("(u p e) k -> p u e k", p=P, e=2),
+            )
+
+        def load_wv(half):
+            cols = slice(half * (H * D // 2), (half + 1) * (H * D // 2))
+            for g in range(HID_PASSES):
+                for u in range(2):
+                    first = g * K_PASS + u * 2 * P
+                    nc.sync.dma_start(
+                        out=wv_in[:, g, 2 * u : 2 * u + 2, cols],
+                        in_=Wv[first : first + 2 * P, cols].rearrange("(p e) c -> p e c", e=2),
+                    )
+
+        def store(group):
+            if not 0 <= group < N_GROUPS:
+                return
+            chunk, head = divmod(group, H)
+            nc.sync.dma_start(
+                out=out_rows[chunk * CHUNK : (chunk + 1) * CHUNK, head * D : (head + 1) * D].rearrange(
+                    "(t p) d -> p t d", p=P
+                ),
+                in_=out_sb[group][:],
+            )
+
+        def transpose_qk(group):
+            if not 0 <= group < N_GROUPS:
+                return
+            for a in range(2):
+                for t in range(QT):
+                    n = a * QT + t
+                    nc.tensor.transpose(
+                        out=side_halves[:, n * P : (n + 1) * P], in_=qk_in[group][:, a, t, :], identity=ident_b[:]
+                    )
+
+        def keep_qk(group):
+            if not 0 <= group < N_GROUPS:
+                return
+            qk_t[group] = qk_t_ring.tile([P, 2, CHUNK], BF16, name="qk_t")
+            nc.vector.tensor_copy(out=qk_t[group][:], in_=side_halves.rearrange("p (a s) -> p a s", a=2))
+
+        def transpose_hs(job):
+            chunk, row_set = job
+            words = hs_in[chunk][:, row_set, :].bitcast(F32)
+            for j in range(4):
+                nc.tensor.transpose(out=side_words[:, j, :], in_=words[:, j * P : (j + 1) * P], identity=ident_f[:])
+
+        def group_hs(job):
+            hs_grouped[job] = hs_grouped_ring.tile([P, HID_PASSES * K_PASS], BF16, name="hs_grouped", align_bytes=64)
+            nc.scalar.copy(
+                out=hs_grouped[job][:].bitcast(F32).rearrange("p (g r u) -> p g r u", r=P, u=2),
+                in_=side_words.rearrange("p (g u) r -> p g r u", u=2),
+            )
+
+        def quantise_hs(job):
+            chunk, row_set = job
+            if row_set == 0:
+                hs_codes[chunk] = hs_mx_ring.tile([P, 4 * HID_PASSES * P], U32, name="hs_codes", align_bytes=64)
+                hs_scales[chunk] = hs_mx_ring.tile([P, 4 * HID_PASSES * P], U8, name="hs_scales", align_bytes=64)
+            cols = slice(row_set * HID_PASSES * P, (row_set + 1) * HID_PASSES * P)
+            nc.vector.quantize_mx(
+                out=hs_codes[chunk][:, cols].bitcast(FP8X4), scales=hs_scales[chunk][:, cols], in_=hs_grouped[job][:]
+            )
+
+        def group_wv(head):
+            if not 0 <= head < H:
+                return
+            wv_grouped[head] = wv_grouped_ring.tile([P, HID_PASSES, D, 4], BF16, name="wv_grouped", align_bytes=64)
+            nc.vector.tensor_copy(
+                out=wv_grouped[head][:],
+                in_=wv_in[:, :, :, head * D : (head + 1) * D].rearrange("p g t c -> p g c t"),
+            )
+
+        def quantise_wv(head):
+            if not 0 <= head < H:
+                return
+            cols = slice(head * HID_PASSES * D, (head + 1) * HID_PASSES * D)
+            nc.vector.quantize_mx(
+                out=wv_codes[:, cols].bitcast(FP8X4),
+                scales=wv_scales[:, cols],
+                in_=wv_grouped[head][:].rearrange("p g c t -> p (g c t)"),
+            )
+
+        def project_v(group):
+            if not 0 <= group < N_GROUPS:
+                return
+            chunk, head = divmod(group, H)
+            for row_set in range(4):
+                for g in range(HID_PASSES):
+                    hs_cols = slice((row_set * HID_PASSES + g) * P, (row_set * HID_PASSES + g + 1) * P)
+                    wv_cols = slice((head * HID_PASSES + g) * D, (head * HID_PASSES + g + 1) * D)
+                    nc.tensor.matmul_mx(
+                        out=side_words[:, row_set, :],
+                        lhsT=hs_codes[chunk][:, hs_cols].bitcast(FP8X4),
+                        lhsT_scale=hs_scales[chunk][:, hs_cols],
+                        rhs=wv_codes[:, wv_cols].bitcast(FP8X4),
+                        rhs_scale=wv_scales[:, wv_cols],
+                        start=(g == 0),
+                        stop=(g == HID_PASSES - 1),
+                    )
+
+        def round_v(group):
+            if not 0 <= group < N_GROUPS:
+                return
+            v_grouped[group] = v_grouped_ring.tile([P, D, 4], BF16, name="v_grouped", align_bytes=64)
+            nc.vector.tensor_copy(out=v_grouped[group][:], in_=side_words.rearrange("p t d -> p d t"))
+
+        def quantise_v(group):
+            if not 0 <= group < N_GROUPS:
+                return
+            chunk, head = divmod(group, H)
+            cols = slice(head * D, (head + 1) * D)
+            nc.vector.quantize_mx(
+                out=v_codes[chunk][:, cols].bitcast(FP8X4),
+                scales=v_scales[chunk][:, cols],
+                in_=v_grouped[group][:].rearrange("p d t -> p (d t)"),
+            )
+
+        def scores(block, own):
+            if not 0 <= block < N_BLOCKS:
+                return
+            group, chunk, head, t = place(block)
+            queries = qk_t[group][:, 0, t * P : (t + 1) * P]
+            bank = score_bank[2 * (block % 2) + own]
+            if own == 0:
+                if chunk > 0:
+                    nc.tensor.matmul(out=bank[:], lhsT=queries, rhs=qk_t[group - H][:, 1, :], start=True, stop=True)
+                return
+            if t > 0:
+                nc.tensor.matmul(
+                    out=bank[:, 0 : t * P], lhsT=queries, rhs=qk_t[group][:, 1, 0 : t * P], start=True, stop=True
+                )
+            diagonal = slice(t * P, (t + 1) * P)
+            nc.tensor.matmul(out=bank[:, diagonal], lhsT=queries, rhs=qk_t[group][:, 1, diagonal], start=True, stop=False)
+            nc.tensor.matmul(out=bank[:, diagonal], lhsT=ident_b[:], rhs=mask_b[:], start=False, stop=True)
+
+        def row_max(block):
+            if not 0 <= block < N_BLOCKS:
+                return
+            group, chunk, head, t = place(block)
+            top[block] = max_ring.tile([P, 2], F32, name="top")
+            if chunk > 0:
+                nc.vector.tensor_reduce(out=top[block][:, 0:1], in_=score_bank[2 * (block % 2)][:], axis=AXIS_X, op=ALU.max)
+            nc.vector.tensor_reduce(
+                out=top[block][:, 1:2], in_=score_bank[2 * (block % 2) + 1][:, 0 : (t + 1) * P], axis=AXIS_X, op=ALU.max
+            )
+
+        def negate_max(block):
+            if not 0 <= block < N_BLOCKS:
+                return
+            group, chunk, head, t = place(block)
+            neg_top[block] = max_ring.tile([P, 1], F32, name="neg_top")
+            if chunk > 0:
+                nc.vector.tensor_scalar(
+                    out=neg_top[block][:], in0=top[block][:, 0:1], scalar1=top[block][:, 1:2], scalar2=-1.0,
+                    op0=ALU.max, op1=ALU.mult,
+                )
+            else:
+                nc.vector.tensor_scalar(
+                    out=neg_top[block][:], in0=top[block][:, 1:2], scalar1=-1.0, scalar2=None, op0=ALU.mult
+                )
+
+        def exponentials(block):
+            if not 0 <= block < N_BLOCKS:
+                return
+            group, chunk, head, t = place(block)
+            if t == 0:
+                row_sum[group] = sum_ring.tile([P, QT, 2], F32, name="row_sum")
+            if chunk > 0:
+                nc.scalar.activation(
+                    out=e_rows[t][:, 0:CHUNK], in_=score_bank[2 * (block % 2)][:], func=ACT.Exp,
+                    bias=neg_top[block][:], scale=1.0, accum_out=row_sum[group][:, t, 0:1],
+                )
+            width = (t + 1) * P
+            nc.scalar.activation(
+                out=e_rows[t][:, CHUNK : CHUNK + width], in_=score_bank[2 * (block % 2) + 1][:, 0:width], func=ACT.Exp,
+                bias=neg_top[block][:], scale=1.0, accum_out=row_sum[group][:, t, 1:2],
+            )
+
+        def add_sums(group):
+            if not H <= group < N_GROUPS:
+                return
+            total[group] = sum_ring.tile([P, QT], F32, name="total")
+            nc.vector.tensor_reduce(out=total[group][:], in_=row_sum[group][:], axis=AXIS_X, op=ALU.add)
+
+        def invert_sums(group):
+            if not 0 <= group < N_GROUPS:
+                return
+            inverse[group] = inverse_ring.tile([P, QT], F32, name="inverse")
+            nc.vector.reciprocal(out=inverse[group][:], in_=total[group][:] if group >= H else row_sum[group][:, :, 1])
+
+        def first_pass(chunk):
+            return 0 if chunk > 0 else 1
+
+        def flip(block):
+            if not 0 <= block < N_BLOCKS:
+                return
+            group, chunk, head, t = place(block)
+            words = e_rows[t][:].bitcast(F32)
+            for j in range(2 * first_pass(chunk), 4):
+                nc.tensor.transpose(
+                    out=flip_bank[block % 2][:, j, :], in_=words[:, j * P : (j + 1) * P], identity=ident_f[:]
+                )
+
+        def group_e(block):
+            if not 0 <= block < N_BLOCKS:
+                return
+            group, chunk, head, t = place(block)
+            g0 = first_pass(chunk)
+            e_grouped[block] = e_grouped_ring.tile([P, 2 * K_PASS], BF16, name="e_grouped", align_bytes=64)
+            nc.scalar.copy(
+                out=e_grouped[block][:].bitcast(F32)[:, g0 * 2 * P : 4 * P].rearrange("p (g r u) -> p g r u", r=P, u=2),
+                in_=flip_bank[block % 2][:, 2 * g0 : 4, :].rearrange("p (g u) r -> p g r u", u=2),
+            )
+
+        def quantise_e(block):
+            if not 0 <= block < N_BLOCKS:
+                return
+            group, chunk, head, t = place(block)
+            g0 = first_pass(chunk)
+            e_codes[block] = e_mx_ring.tile([P, 2 * P], U32, name="e_codes", align_bytes=64)
+            e_scales[block] = e_mx_ring.tile([P, 2 * P], U8, name="e_scales", align_bytes=64)
+            nc.vector.quantize_mx(
+                out=e_codes[block][:, g0 * P : 2 * P].bitcast(FP8X4),
+                scales=e_scales[block][:, g0 * P : 2 * P],
+                in_=e_grouped[block][:, g0 * K_PASS : 2 * K_PASS],
+            )
+
+        def attend(block):
+            if not 0 <= block < N_BLOCKS:
+                return
+            group, chunk, head, t = place(block)
+            for g in range(first_pass(chunk), 2):
+                nc.tensor.matmul_mx(
+                    out=out_bank[:, t, :],
+                    lhsT=e_codes[block][:, g * P : (g + 1) * P].bitcast(FP8X4),
+                    lhsT_scale=e_scales[block][:, g * P : (g + 1) * P],
+                    rhs=v_codes[chunk - 1 + g][:, head * D : (head + 1) * D].bitcast(FP8X4),
+                    rhs_scale=v_scales[chunk - 1 + g][:, head * D : (head + 1) * D],
+                    start=(g == first_pass(chunk)),
+                    stop=(g == 1),
+                )
+
+        def normalise(block):
+            if not 0 <= block < N_BLOCKS:
+                return
+            group, chunk, head, t = place(block)
+            if t == 0:
+                out_sb[group] = out_ring.tile([P, QT, D], F32, name="out_sb")
+            nc.scalar.activation(
+                out=out_sb[group][:, t, :], in_=out_bank[:, t, :], func=ACT.Copy, scale=inverse[group][:, t : t + 1]
+            )
+
+        load_qk(0)
+        load_qk(1)
+        load_hs(0)
+        load_qk(2)
+        load_wv(0)
+        load_qk(3)
+        load_wv(1)
+        load_hs(1)
+
+        make_identity(nc, ident_b[:])
+        make_identity(nc, ident_f[:])
+        nc.gpsimd.memset(mask_f[:], 0.0)
+        nc.gpsimd.affine_select(
+            out=mask_f[:], in_=mask_f[:], compare_op=ALU.is_ge, fill=MASK_VALUE, base=0, pattern=[[-1, P]],
+            channel_multiplier=1,
+        )
+        nc.vector.tensor_copy(out=mask_b[:], in_=mask_f[:])
+        for t in range(QT - 1):
+            nc.vector.memset(e_rows[t][:, CHUNK + (t + 1) * P : 2 * CHUNK], 0.0)
+
+        for tick in range(-QT, N_BLOCKS + LAG + 1 + 1):
+            group_now, phase = divmod(tick, QT)
+            row_max(tick + 1)
+            exponentials(tick)
+            flip(tick - 1)
+            attend(tick - LAG)
+            if phase == 0:
+                transpose_qk(group_now + 1)
+            if phase == 1:
+                project_v(group_now - V_BEHIND)
+            if hs_job(tick) is not None:
+                transpose_hs(hs_job(tick))
+                group_hs(hs_job(tick))
+            scores(tick + 2, 0)
+            scores(tick + 2, 1)
+            group_e(tick - 1)
+            normalise(tick - LAG - 1)
+            quantise_e(tick - 2)
+            negate_max(tick + 1)
+            if hs_job(tick - 1) is not None:
+                quantise_hs(hs_job(tick - 1))
+            if phase == 0:
+                keep_qk(group_now + 1)
+                quantise_wv(group_now - V_BEHIND)
+                add_sums(group_now - 1)
+                store(group_now - LAG // QT - 1)
+            if phase == 1:
+                round_v(group_now - V_BEHIND)
+                invert_sums(group_now - 1)
+                load_qk(group_now + QK_AHEAD)
+                if group_now % H == 2:
+                    load_hs(group_now // H + 2)
+            if phase == 2:
+                quantise_v(group_now - V_BEHIND)
+            if phase == 3:
+                group_wv(group_now - V_BEHIND + 1)

@@ -23,8 +23,10 @@ N_BLOCKS = N_GROUPS * QT
 HID_PASSES = HID // K_PASS
 
 LAG = 12
-V_BEHIND = LAG // QT - 1
+BEHIND = LAG // QT
 QK_AHEAD = 5
+LIFT_AHEAD = 2
+FIRST_TICK = -3 * QT
 
 FLOPS = 2 * S * HID * H * D + 2 * (2 * H * D * CHUNK * (CHUNK + (N_CHUNKS - 1) * 2 * CHUNK))
 
@@ -35,11 +37,10 @@ def place(block):
     return group, chunk, head, t
 
 
-def hs_job(tick):
-    group, phase = divmod(tick, QT)
-    chunk, head = divmod(group, H)
-    if 0 <= chunk < N_CHUNKS and head < 2 and phase >= 2:
-        return chunk, 2 * head + phase - 2
+def hs_job(group):
+    chunk, row_set = divmod(group + 3, H)
+    if 0 <= chunk < N_CHUNKS and row_set < 4:
+        return chunk, row_set
     return None
 
 
@@ -61,7 +62,7 @@ def tile_localselfattention_pa_kernel(tc, q, k_scaled, hidden_states, Wv, out):
 
         score_bank = [banks.tile([P, CHUNK], F32, name="score_bank%d" % n) for n in range(4)]
         flip_bank = [banks.tile([P, 4, P], F32, name="flip_bank%d" % n) for n in range(2)]
-        out_bank = banks.tile([P, QT, D], F32, name="out_bank")
+        mx_bank = banks.tile([P, 4, P], F32, name="mx_bank")
         side_bank = banks.tile([P, 4 * P], F32, name="side_bank")
         side_words = side_bank[:].rearrange("p (j r) -> p j r", r=P)
         side_halves = side_bank[:].bitcast(BF16)
@@ -85,15 +86,15 @@ def tile_localselfattention_pa_kernel(tc, q, k_scaled, hidden_states, Wv, out):
         hs_mx_ring = ring("hs_mx", 2)
         wv_grouped_ring = ring("wv_grouped", 2)
         v_grouped_ring = ring("v_grouped", 2)
-        max_ring = ring("max", 3)
+        lifted_ring = ring("lifted", LIFT_AHEAD + 2)
         sum_ring = ring("sum", 3)
-        inverse_ring = ring("inverse", LAG // QT + 2)
+        inverse_ring = ring("inverse", BEHIND + 1)
         e_grouped_ring = ring("e_grouped", 3)
         e_mx_ring = ring("e_mx", LAG)
         out_ring = ring("out", 3)
 
         qk_in, qk_t, hs_in, hs_grouped, hs_codes, hs_scales = {}, {}, {}, {}, {}, {}
-        wv_grouped, v_grouped, top, neg_top, row_sum, total, inverse = {}, {}, {}, {}, {}, {}, {}
+        wv_grouped, v_grouped, lifted, neg_back, neg_top, row_sum, total, inverse = {}, {}, {}, {}, {}, {}, {}, {}
         e_grouped, e_codes, e_scales, out_sb = {}, {}, {}, {}
 
         def load_qk(group):
@@ -105,16 +106,17 @@ def tile_localselfattention_pa_kernel(tc, q, k_scaled, hidden_states, Wv, out):
             nc.sync.dma_start(out=qk_in[group][:, 0], in_=q_rows[rows, :].rearrange("(t p) d -> p t d", p=P))
             nc.sync.dma_start(out=qk_in[group][:, 1], in_=k_rows[rows, :].rearrange("(t p) d -> p t d", p=P))
 
-        def load_hs(chunk):
+        def load_hs(chunk, row_set):
             if not 0 <= chunk < N_CHUNKS:
                 return
-            hs_in[chunk] = hs_in_ring.tile([P, 4, HID], BF16, name="hs_in")
-            nc.sync.dma_start(
-                out=hs_in[chunk][:].rearrange("p (u e) k -> p u e k", e=2),
-                in_=hs_rows[chunk * CHUNK : (chunk + 1) * CHUNK, :].rearrange("(u p e) k -> p u e k", p=P, e=2),
-            )
+            if row_set == 0:
+                hs_in[chunk] = hs_in_ring.tile([P, 4, HID], BF16, name="hs_in")
+            by_set = hs_rows[chunk * CHUNK : (chunk + 1) * CHUNK, :].rearrange("(u p e) k -> p u e k", p=P, e=2)
+            nc.sync.dma_start(out=hs_in[chunk][:, row_set, :], in_=by_set[:, row_set // 2, row_set % 2, :])
 
         def load_wv(half):
+            if not 0 <= half < 2:
+                return
             cols = slice(half * (H * D // 2), (half + 1) * (H * D // 2))
             for g in range(HID_PASSES):
                 for u in range(2):
@@ -152,12 +154,16 @@ def tile_localselfattention_pa_kernel(tc, q, k_scaled, hidden_states, Wv, out):
             nc.vector.tensor_copy(out=qk_t[group][:], in_=side_halves.rearrange("p (a s) -> p a s", a=2))
 
         def transpose_hs(job):
+            if job is None:
+                return
             chunk, row_set = job
             words = hs_in[chunk][:, row_set, :].bitcast(F32)
             for j in range(4):
                 nc.tensor.transpose(out=side_words[:, j, :], in_=words[:, j * P : (j + 1) * P], identity=ident_f[:])
 
         def group_hs(job):
+            if job is None:
+                return
             hs_grouped[job] = hs_grouped_ring.tile([P, HID_PASSES * K_PASS], BF16, name="hs_grouped", align_bytes=64)
             nc.scalar.copy(
                 out=hs_grouped[job][:].bitcast(F32).rearrange("p (g r u) -> p g r u", r=P, u=2),
@@ -165,6 +171,8 @@ def tile_localselfattention_pa_kernel(tc, q, k_scaled, hidden_states, Wv, out):
             )
 
         def quantise_hs(job):
+            if job is None:
+                return
             chunk, row_set = job
             if row_set == 0:
                 hs_codes[chunk] = hs_mx_ring.tile([P, 4 * HID_PASSES * P], U32, name="hs_codes", align_bytes=64)
@@ -178,7 +186,7 @@ def tile_localselfattention_pa_kernel(tc, q, k_scaled, hidden_states, Wv, out):
             if not 0 <= head < H:
                 return
             wv_grouped[head] = wv_grouped_ring.tile([P, HID_PASSES, D, 4], BF16, name="wv_grouped", align_bytes=64)
-            nc.vector.tensor_copy(
+            nc.scalar.copy(
                 out=wv_grouped[head][:],
                 in_=wv_in[:, :, :, head * D : (head + 1) * D].rearrange("p g t c -> p g c t"),
             )
@@ -202,7 +210,7 @@ def tile_localselfattention_pa_kernel(tc, q, k_scaled, hidden_states, Wv, out):
                     hs_cols = slice((row_set * HID_PASSES + g) * P, (row_set * HID_PASSES + g + 1) * P)
                     wv_cols = slice((head * HID_PASSES + g) * D, (head * HID_PASSES + g + 1) * D)
                     nc.tensor.matmul_mx(
-                        out=side_words[:, row_set, :],
+                        out=mx_bank[:, row_set, :],
                         lhsT=hs_codes[chunk][:, hs_cols].bitcast(FP8X4),
                         lhsT_scale=hs_scales[chunk][:, hs_cols],
                         rhs=wv_codes[:, wv_cols].bitcast(FP8X4),
@@ -215,7 +223,7 @@ def tile_localselfattention_pa_kernel(tc, q, k_scaled, hidden_states, Wv, out):
             if not 0 <= group < N_GROUPS:
                 return
             v_grouped[group] = v_grouped_ring.tile([P, D, 4], BF16, name="v_grouped", align_bytes=64)
-            nc.vector.tensor_copy(out=v_grouped[group][:], in_=side_words.rearrange("p t d -> p d t"))
+            nc.vector.tensor_copy(out=v_grouped[group][:], in_=mx_bank[:].rearrange("p t d -> p d t"))
 
         def quantise_v(group):
             if not 0 <= group < N_GROUPS:
@@ -228,49 +236,45 @@ def tile_localselfattention_pa_kernel(tc, q, k_scaled, hidden_states, Wv, out):
                 in_=v_grouped[group][:].rearrange("p d t -> p (d t)"),
             )
 
-        def scores(block, own):
+        def scores(block):
             if not 0 <= block < N_BLOCKS:
                 return
             group, chunk, head, t = place(block)
             queries = qk_t[group][:, 0, t * P : (t + 1) * P]
-            bank = score_bank[2 * (block % 2) + own]
-            if own == 0:
-                if chunk > 0:
-                    nc.tensor.matmul(out=bank[:], lhsT=queries, rhs=qk_t[group - H][:, 1, :], start=True, stop=True)
-                return
+            back, own = score_bank[2 * (block % 2)], score_bank[2 * (block % 2) + 1]
+            if chunk > 0:
+                nc.tensor.matmul(out=back[:], lhsT=queries, rhs=qk_t[group - H][:, 1, :], start=True, stop=True)
             if t > 0:
                 nc.tensor.matmul(
-                    out=bank[:, 0 : t * P], lhsT=queries, rhs=qk_t[group][:, 1, 0 : t * P], start=True, stop=True
+                    out=own[:, 0 : t * P], lhsT=queries, rhs=qk_t[group][:, 1, 0 : t * P], start=True, stop=True
                 )
             diagonal = slice(t * P, (t + 1) * P)
-            nc.tensor.matmul(out=bank[:, diagonal], lhsT=queries, rhs=qk_t[group][:, 1, diagonal], start=True, stop=False)
-            nc.tensor.matmul(out=bank[:, diagonal], lhsT=ident_b[:], rhs=mask_b[:], start=False, stop=True)
+            nc.tensor.matmul(out=own[:, diagonal], lhsT=queries, rhs=qk_t[group][:, 1, diagonal], start=True, stop=False)
+            nc.tensor.matmul(out=own[:, diagonal], lhsT=ident_b[:], rhs=mask_b[:], start=False, stop=True)
 
-        def row_max(block):
-            if not 0 <= block < N_BLOCKS:
+        def lift_back(block):
+            if not H * QT <= block < N_BLOCKS:
                 return
-            group, chunk, head, t = place(block)
-            top[block] = max_ring.tile([P, 2], F32, name="top")
-            if chunk > 0:
-                nc.vector.tensor_reduce(out=top[block][:, 0:1], in_=score_bank[2 * (block % 2)][:], axis=AXIS_X, op=ALU.max)
-            nc.vector.tensor_reduce(
-                out=top[block][:, 1:2], in_=score_bank[2 * (block % 2) + 1][:, 0 : (t + 1) * P], axis=AXIS_X, op=ALU.max
+            lifted[block] = lifted_ring.tile([P, 2 * CHUNK], F32, name="lifted")
+            neg_back[block] = lifted_ring.tile([P, 1], F32, name="neg_back")
+            nc.vector.tensor_scalar(
+                out=lifted[block][:, 0:CHUNK], in0=score_bank[2 * (block % 2)][:], scalar1=-1.0, scalar2=None,
+                op0=ALU.mult, op1=ALU.min, accum_out=neg_back[block][:],
             )
 
-        def negate_max(block):
+        def lift_own(block):
             if not 0 <= block < N_BLOCKS:
                 return
             group, chunk, head, t = place(block)
-            neg_top[block] = max_ring.tile([P, 1], F32, name="neg_top")
-            if chunk > 0:
-                nc.vector.tensor_scalar(
-                    out=neg_top[block][:], in0=top[block][:, 0:1], scalar1=top[block][:, 1:2], scalar2=-1.0,
-                    op0=ALU.max, op1=ALU.mult,
-                )
-            else:
-                nc.vector.tensor_scalar(
-                    out=neg_top[block][:], in0=top[block][:, 1:2], scalar1=-1.0, scalar2=None, op0=ALU.mult
-                )
+            if chunk == 0:
+                lifted[block] = lifted_ring.tile([P, 2 * CHUNK], F32, name="lifted")
+            neg_top[block] = lifted_ring.tile([P, 1], F32, name="neg_top")
+            width = (t + 1) * P
+            nc.vector.tensor_scalar(
+                out=lifted[block][:, CHUNK : CHUNK + width], in0=score_bank[2 * (block % 2) + 1][:, 0:width],
+                scalar1=-1.0, scalar2=neg_back[block][:] if chunk > 0 else None,
+                op0=ALU.mult, op1=ALU.min, accum_out=neg_top[block][:],
+            )
 
         def exponentials(block):
             if not 0 <= block < N_BLOCKS:
@@ -280,13 +284,13 @@ def tile_localselfattention_pa_kernel(tc, q, k_scaled, hidden_states, Wv, out):
                 row_sum[group] = sum_ring.tile([P, QT, 2], F32, name="row_sum")
             if chunk > 0:
                 nc.scalar.activation(
-                    out=e_rows[t][:, 0:CHUNK], in_=score_bank[2 * (block % 2)][:], func=ACT.Exp,
-                    bias=neg_top[block][:], scale=1.0, accum_out=row_sum[group][:, t, 0:1],
+                    out=e_rows[t][:, 0:CHUNK], in_=lifted[block][:, 0:CHUNK], func=ACT.Exp,
+                    bias=neg_top[block][:], scale=-1.0, accum_out=row_sum[group][:, t, 0:1],
                 )
-            width = (t + 1) * P
+            own = slice(CHUNK, CHUNK + (t + 1) * P)
             nc.scalar.activation(
-                out=e_rows[t][:, CHUNK : CHUNK + width], in_=score_bank[2 * (block % 2) + 1][:, 0:width], func=ACT.Exp,
-                bias=neg_top[block][:], scale=1.0, accum_out=row_sum[group][:, t, 1:2],
+                out=e_rows[t][:, own], in_=lifted[block][:, own], func=ACT.Exp,
+                bias=neg_top[block][:], scale=-1.0, accum_out=row_sum[group][:, t, 1:2],
             )
 
         def add_sums(group):
@@ -338,42 +342,41 @@ def tile_localselfattention_pa_kernel(tc, q, k_scaled, hidden_states, Wv, out):
                 in_=e_grouped[block][:, g0 * K_PASS : 2 * K_PASS],
             )
 
-        def attend(block):
-            if not 0 <= block < N_BLOCKS:
+        def attend(group):
+            if not 0 <= group < N_GROUPS:
                 return
-            group, chunk, head, t = place(block)
-            for g in range(first_pass(chunk), 2):
-                nc.tensor.matmul_mx(
-                    out=out_bank[:, t, :],
-                    lhsT=e_codes[block][:, g * P : (g + 1) * P].bitcast(FP8X4),
-                    lhsT_scale=e_scales[block][:, g * P : (g + 1) * P],
-                    rhs=v_codes[chunk - 1 + g][:, head * D : (head + 1) * D].bitcast(FP8X4),
-                    rhs_scale=v_scales[chunk - 1 + g][:, head * D : (head + 1) * D],
-                    start=(g == first_pass(chunk)),
-                    stop=(g == 1),
+            chunk, head = divmod(group, H)
+            for t in range(QT):
+                block = group * QT + t
+                for g in range(first_pass(chunk), 2):
+                    nc.tensor.matmul_mx(
+                        out=mx_bank[:, t, :],
+                        lhsT=e_codes[block][:, g * P : (g + 1) * P].bitcast(FP8X4),
+                        lhsT_scale=e_scales[block][:, g * P : (g + 1) * P],
+                        rhs=v_codes[chunk - 1 + g][:, head * D : (head + 1) * D].bitcast(FP8X4),
+                        rhs_scale=v_scales[chunk - 1 + g][:, head * D : (head + 1) * D],
+                        start=(g == first_pass(chunk)),
+                        stop=(g == 1),
+                    )
+
+        def normalise(group):
+            if not 0 <= group < N_GROUPS:
+                return
+            out_sb[group] = out_ring.tile([P, QT, D], F32, name="out_sb")
+            for t in range(QT):
+                nc.scalar.activation(
+                    out=out_sb[group][:, t, :], in_=mx_bank[:, t, :], func=ACT.Copy, scale=inverse[group][:, t : t + 1]
                 )
 
-        def normalise(block):
-            if not 0 <= block < N_BLOCKS:
-                return
-            group, chunk, head, t = place(block)
-            if t == 0:
-                out_sb[group] = out_ring.tile([P, QT, D], F32, name="out_sb")
-            nc.scalar.activation(
-                out=out_sb[group][:, t, :], in_=out_bank[:, t, :], func=ACT.Copy, scale=inverse[group][:, t : t + 1]
-            )
-
+        load_hs(0, 0)
         load_qk(0)
+        load_hs(0, 1)
         load_qk(1)
-        load_hs(0)
-        load_qk(2)
-        load_wv(0)
-        load_qk(3)
-        load_wv(1)
-        load_hs(1)
+        load_hs(0, 2)
+        load_hs(0, 3)
 
-        make_identity(nc, ident_b[:])
         make_identity(nc, ident_f[:])
+        make_identity(nc, ident_b[:])
         nc.gpsimd.memset(mask_f[:], 0.0)
         nc.gpsimd.affine_select(
             out=mask_f[:], in_=mask_f[:], compare_op=ALU.is_ge, fill=MASK_VALUE, base=0, pattern=[[-1, P]],
@@ -383,39 +386,36 @@ def tile_localselfattention_pa_kernel(tc, q, k_scaled, hidden_states, Wv, out):
         for t in range(QT - 1):
             nc.vector.memset(e_rows[t][:, CHUNK + (t + 1) * P : 2 * CHUNK], 0.0)
 
-        for tick in range(-QT, N_BLOCKS + LAG + 1 + 1):
+        for tick in range(FIRST_TICK, (N_GROUPS - 1) * QT + LAG + 2):
             group_now, phase = divmod(tick, QT)
-            row_max(tick + 1)
+            lift_back(tick + LIFT_AHEAD)
+            quantise_e(tick - 3)
+            lift_own(tick + LIFT_AHEAD)
+            group_e(tick - 2)
             exponentials(tick)
             flip(tick - 1)
-            attend(tick - LAG)
             if phase == 0:
-                transpose_qk(group_now + 1)
-            if phase == 1:
-                project_v(group_now - V_BEHIND)
-            if hs_job(tick) is not None:
-                transpose_hs(hs_job(tick))
-                group_hs(hs_job(tick))
-            scores(tick + 2, 0)
-            scores(tick + 2, 1)
-            group_e(tick - 1)
-            normalise(tick - LAG - 1)
-            quantise_e(tick - 2)
-            negate_max(tick + 1)
-            if hs_job(tick - 1) is not None:
-                quantise_hs(hs_job(tick - 1))
-            if phase == 0:
-                keep_qk(group_now + 1)
-                quantise_wv(group_now - V_BEHIND)
+                attend(group_now - BEHIND)
+                group_hs(hs_job(group_now - 1))
+                group_wv(group_now - BEHIND + 2)
+                quantise_v(group_now - BEHIND + 1)
                 add_sums(group_now - 1)
-                store(group_now - LAG // QT - 1)
             if phase == 1:
-                round_v(group_now - V_BEHIND)
+                normalise(group_now - BEHIND)
+                store(group_now - BEHIND)
+                transpose_qk(group_now + 2)
+                quantise_hs(hs_job(group_now - 1))
+                quantise_wv(group_now - BEHIND + 2)
                 invert_sums(group_now - 1)
                 load_qk(group_now + QK_AHEAD)
-                if group_now % H == 2:
-                    load_hs(group_now // H + 2)
+                load_wv(group_now + 3)
+                if (group_now + 1) % H == 0:
+                    for row_set in range(4):
+                        load_hs((group_now + 1) // H + 1, row_set)
             if phase == 2:
-                quantise_v(group_now - V_BEHIND)
+                project_v(group_now - BEHIND + 2)
+                keep_qk(group_now + 2)
             if phase == 3:
-                group_wv(group_now - V_BEHIND + 1)
+                round_v(group_now - BEHIND + 2)
+                transpose_hs(hs_job(group_now))
+            scores(tick + LIFT_AHEAD + 2)

@@ -10,7 +10,6 @@ U8 = mybir.dt.uint8
 FP8X4 = mybir.dt.float8_e4m3fn_x4
 ACT = mybir.ActivationFunctionType
 ALU = mybir.AluOpType
-AXIS_X = mybir.AxisListType.X
 
 P = 128
 S, HID, H, D, CHUNK = 2048, 1024, 8, 128, 512
@@ -94,7 +93,7 @@ def tile_localselfattention_pa_kernel(tc, q, k_scaled, hidden_states, Wv, out):
         out_ring = ring("out", 3)
 
         qk_in, qk_t, hs_in, hs_grouped, hs_codes, hs_scales = {}, {}, {}, {}, {}, {}
-        wv_grouped, v_grouped, lifted, neg_back, neg_top, row_sum, total, inverse = {}, {}, {}, {}, {}, {}, {}, {}
+        wv_grouped, v_grouped, lifted, neg_back, neg_top, row_sum, inverse = {}, {}, {}, {}, {}, {}, {}
         e_grouped, e_codes, e_scales, out_sb = {}, {}, {}, {}
 
         def load_qk(group):
@@ -281,29 +280,18 @@ def tile_localselfattention_pa_kernel(tc, q, k_scaled, hidden_states, Wv, out):
                 return
             group, chunk, head, t = place(block)
             if t == 0:
-                row_sum[group] = sum_ring.tile([P, QT, 2], F32, name="row_sum")
-            if chunk > 0:
-                nc.scalar.activation(
-                    out=e_rows[t][:, 0:CHUNK], in_=lifted[block][:, 0:CHUNK], func=ACT.Exp,
-                    bias=neg_top[block][:], scale=-1.0, accum_out=row_sum[group][:, t, 0:1],
-                )
-            own = slice(CHUNK, CHUNK + (t + 1) * P)
+                row_sum[group] = sum_ring.tile([P, QT], F32, name="row_sum")
+            keys = slice(0 if chunk > 0 else CHUNK, CHUNK + (t + 1) * P)
             nc.scalar.activation(
-                out=e_rows[t][:, own], in_=lifted[block][:, own], func=ACT.Exp,
-                bias=neg_top[block][:], scale=-1.0, accum_out=row_sum[group][:, t, 1:2],
+                out=e_rows[t][:, keys], in_=lifted[block][:, keys], func=ACT.Exp,
+                bias=neg_top[block][:], scale=-1.0, accum_out=row_sum[group][:, t : t + 1],
             )
-
-        def add_sums(group):
-            if not H <= group < N_GROUPS:
-                return
-            total[group] = sum_ring.tile([P, QT], F32, name="total")
-            nc.vector.tensor_reduce(out=total[group][:], in_=row_sum[group][:], axis=AXIS_X, op=ALU.add)
 
         def invert_sums(group):
             if not 0 <= group < N_GROUPS:
                 return
             inverse[group] = inverse_ring.tile([P, QT], F32, name="inverse")
-            nc.vector.reciprocal(out=inverse[group][:], in_=total[group][:] if group >= H else row_sum[group][:, :, 1])
+            nc.vector.reciprocal(out=inverse[group][:], in_=row_sum[group][:])
 
         def first_pass(chunk):
             return 0 if chunk > 0 else 1
@@ -399,7 +387,6 @@ def tile_localselfattention_pa_kernel(tc, q, k_scaled, hidden_states, Wv, out):
                 group_hs(hs_job(group_now - 1))
                 group_wv(group_now - BEHIND + 2)
                 quantise_v(group_now - BEHIND + 1)
-                add_sums(group_now - 1)
             if phase == 1:
                 normalise(group_now - BEHIND)
                 store(group_now - BEHIND)

@@ -85,7 +85,7 @@ def tile_localselfattention_pa_kernel(tc, q, k_scaled, hidden_states, Wv, out):
         hs_mx_ring = ring("hs_mx", 2)
         wv_grouped_ring = ring("wv_grouped", 2)
         v_grouped_ring = ring("v_grouped", 2)
-        lifted_ring = ring("lifted", LIFT_AHEAD + 2)
+        lifted_ring = ring("lifted", LIFT_AHEAD + 3)
         sum_ring = ring("sum", 3)
         inverse_ring = ring("inverse", BEHIND + 1)
         e_grouped_ring = ring("e_grouped", 3)
@@ -93,7 +93,7 @@ def tile_localselfattention_pa_kernel(tc, q, k_scaled, hidden_states, Wv, out):
         out_ring = ring("out", 3)
 
         qk_in, qk_t, hs_in, hs_grouped, hs_codes, hs_scales = {}, {}, {}, {}, {}, {}
-        wv_grouped, v_grouped, lifted, neg_back, neg_top, row_sum, inverse = {}, {}, {}, {}, {}, {}, {}
+        wv_grouped, v_grouped, lifted, neg_own, neg_top, row_sum, inverse = {}, {}, {}, {}, {}, {}, {}
         e_grouped, e_codes, e_scales, out_sb = {}, {}, {}, {}
 
         def load_qk(group):
@@ -251,28 +251,28 @@ def tile_localselfattention_pa_kernel(tc, q, k_scaled, hidden_states, Wv, out):
             nc.tensor.matmul(out=own[:, diagonal], lhsT=queries, rhs=qk_t[group][:, 1, diagonal], start=True, stop=False)
             nc.tensor.matmul(out=own[:, diagonal], lhsT=ident_b[:], rhs=mask_b[:], start=False, stop=True)
 
-        def lift_back(block):
-            if not H * QT <= block < N_BLOCKS:
-                return
-            lifted[block] = lifted_ring.tile([P, 2 * CHUNK], F32, name="lifted")
-            neg_back[block] = lifted_ring.tile([P, 1], F32, name="neg_back")
-            nc.vector.tensor_scalar(
-                out=lifted[block][:, 0:CHUNK], in0=score_bank[2 * (block % 2)][:], scalar1=-1.0, scalar2=None,
-                op0=ALU.mult, op1=ALU.min, accum_out=neg_back[block][:],
-            )
-
         def lift_own(block):
             if not 0 <= block < N_BLOCKS:
                 return
             group, chunk, head, t = place(block)
-            if chunk == 0:
-                lifted[block] = lifted_ring.tile([P, 2 * CHUNK], F32, name="lifted")
-            neg_top[block] = lifted_ring.tile([P, 1], F32, name="neg_top")
+            lifted[block] = lifted_ring.tile([P, 2 * CHUNK], F32, name="lifted")
+            neg_own[block] = lifted_ring.tile([P, 1], F32, name="neg_own")
             width = (t + 1) * P
             nc.vector.tensor_scalar(
                 out=lifted[block][:, CHUNK : CHUNK + width], in0=score_bank[2 * (block % 2) + 1][:, 0:width],
-                scalar1=-1.0, scalar2=neg_back[block][:] if chunk > 0 else None,
-                op0=ALU.mult, op1=ALU.min, accum_out=neg_top[block][:],
+                scalar1=-1.0, scalar2=None, op0=ALU.mult, op1=ALU.min, accum_out=neg_own[block][:],
+            )
+
+        def lift_back(block):
+            if not 0 <= block < N_BLOCKS:
+                return
+            if block < H * QT:
+                neg_top[block] = neg_own[block]
+                return
+            neg_top[block] = lifted_ring.tile([P, 1], F32, name="neg_top")
+            nc.vector.tensor_scalar(
+                out=lifted[block][:, 0:CHUNK], in0=score_bank[2 * (block % 2)][:], scalar1=-1.0,
+                scalar2=neg_own[block][:], op0=ALU.mult, op1=ALU.min, accum_out=neg_top[block][:],
             )
 
         def exponentials(block):
@@ -376,9 +376,9 @@ def tile_localselfattention_pa_kernel(tc, q, k_scaled, hidden_states, Wv, out):
 
         for tick in range(FIRST_TICK, (N_GROUPS - 1) * QT + LAG + 2):
             group_now, phase = divmod(tick, QT)
-            lift_back(tick + LIFT_AHEAD)
-            quantise_e(tick - 3)
             lift_own(tick + LIFT_AHEAD)
+            quantise_e(tick - 3)
+            lift_back(tick + LIFT_AHEAD)
             group_e(tick - 2)
             exponentials(tick)
             flip(tick - 1)

@@ -21,19 +21,18 @@ N_GROUPS = N_CHUNKS * H
 N_BLOCKS = N_GROUPS * QT
 HID_PASSES = HID // K_PASS
 
-LAG = 12
-BEHIND = LAG // QT
+BEHIND = 3
 QK_AHEAD = 5
-LIFT_AHEAD = 2
-FIRST_TICK = -3 * QT
+FIRST_STEP = -5
+BLOCK_ORDER = (0, 2, 1, 3)
 
 FLOPS = 2 * S * HID * H * D + 2 * (2 * H * D * CHUNK * (CHUNK + (N_CHUNKS - 1) * 2 * CHUNK))
 
 
 def place(block):
-    group, t = divmod(block, QT)
+    group, n = divmod(block, QT)
     chunk, head = divmod(group, H)
-    return group, chunk, head, t
+    return group, chunk, head, BLOCK_ORDER[n]
 
 
 def hs_job(group):
@@ -61,10 +60,10 @@ def tile_localselfattention_pa_kernel(tc, q, k_scaled, hidden_states, Wv, out):
 
         score_bank = [banks.tile([P, CHUNK], F32, name="score_bank%d" % n) for n in range(4)]
         flip_bank = [banks.tile([P, 4, P], F32, name="flip_bank%d" % n) for n in range(2)]
-        mx_bank = banks.tile([P, 4, P], F32, name="mx_bank")
-        side_bank = banks.tile([P, 4 * P], F32, name="side_bank")
-        side_words = side_bank[:].rearrange("p (j r) -> p j r", r=P)
-        side_halves = side_bank[:].bitcast(BF16)
+        attend_bank = banks.tile([P, 4 * P], F32, name="attend_bank")
+        attend_sums = attend_bank[:].rearrange("p (t d) -> p t d", d=D)
+        attend_halves = attend_bank[:].bitcast(BF16)
+        project_bank = banks.tile([P, 4, P], F32, name="project_bank")
 
         ident_f = fixed.tile([P, P], F32, name="ident_f")
         ident_b = fixed.tile([P, P], BF16, name="ident_b")
@@ -85,11 +84,11 @@ def tile_localselfattention_pa_kernel(tc, q, k_scaled, hidden_states, Wv, out):
         hs_mx_ring = ring("hs_mx", 2)
         wv_grouped_ring = ring("wv_grouped", 2)
         v_grouped_ring = ring("v_grouped", 2)
-        lifted_ring = ring("lifted", LIFT_AHEAD + 3)
+        lifted_ring = ring("lifted", 6)
         sum_ring = ring("sum", 3)
         inverse_ring = ring("inverse", BEHIND + 1)
-        e_grouped_ring = ring("e_grouped", 3)
-        e_mx_ring = ring("e_mx", LAG)
+        e_grouped_ring = ring("e_grouped", 5)
+        e_mx_ring = ring("e_mx", BEHIND * QT)
         out_ring = ring("out", 3)
 
         qk_in, qk_t, hs_in, hs_grouped, hs_codes, hs_scales = {}, {}, {}, {}, {}, {}
@@ -143,14 +142,14 @@ def tile_localselfattention_pa_kernel(tc, q, k_scaled, hidden_states, Wv, out):
                 for t in range(QT):
                     n = a * QT + t
                     nc.tensor.transpose(
-                        out=side_halves[:, n * P : (n + 1) * P], in_=qk_in[group][:, a, t, :], identity=ident_b[:]
+                        out=attend_halves[:, n * P : (n + 1) * P], in_=qk_in[group][:, a, t, :], identity=ident_b[:]
                     )
 
         def keep_qk(group):
             if not 0 <= group < N_GROUPS:
                 return
             qk_t[group] = qk_t_ring.tile([P, 2, CHUNK], BF16, name="qk_t")
-            nc.vector.tensor_copy(out=qk_t[group][:], in_=side_halves.rearrange("p (a s) -> p a s", a=2))
+            nc.vector.tensor_copy(out=qk_t[group][:], in_=attend_halves.rearrange("p (a s) -> p a s", a=2))
 
         def transpose_hs(job):
             if job is None:
@@ -158,7 +157,7 @@ def tile_localselfattention_pa_kernel(tc, q, k_scaled, hidden_states, Wv, out):
             chunk, row_set = job
             words = hs_in[chunk][:, row_set, :].bitcast(F32)
             for j in range(4):
-                nc.tensor.transpose(out=side_words[:, j, :], in_=words[:, j * P : (j + 1) * P], identity=ident_f[:])
+                nc.tensor.transpose(out=project_bank[:, j, :], in_=words[:, j * P : (j + 1) * P], identity=ident_f[:])
 
         def group_hs(job):
             if job is None:
@@ -166,7 +165,7 @@ def tile_localselfattention_pa_kernel(tc, q, k_scaled, hidden_states, Wv, out):
             hs_grouped[job] = hs_grouped_ring.tile([P, HID_PASSES * K_PASS], BF16, name="hs_grouped", align_bytes=64)
             nc.scalar.copy(
                 out=hs_grouped[job][:].bitcast(F32).rearrange("p (g r u) -> p g r u", r=P, u=2),
-                in_=side_words.rearrange("p (g u) r -> p g r u", u=2),
+                in_=project_bank[:].rearrange("p (g u) r -> p g r u", u=2),
             )
 
         def quantise_hs(job):
@@ -185,10 +184,12 @@ def tile_localselfattention_pa_kernel(tc, q, k_scaled, hidden_states, Wv, out):
             if not 0 <= head < H:
                 return
             wv_grouped[head] = wv_grouped_ring.tile([P, HID_PASSES, D, 4], BF16, name="wv_grouped", align_bytes=64)
-            nc.scalar.copy(
-                out=wv_grouped[head][:],
-                in_=wv_in[:, :, :, head * D : (head + 1) * D].rearrange("p g t c -> p g c t"),
-            )
+            for g in range(HID_PASSES):
+                nc.gpsimd.tensor_scalar(
+                    out=wv_grouped[head][:, g],
+                    in0=wv_in[:, g, :, head * D : (head + 1) * D].rearrange("p t c -> p c t"),
+                    scalar1=1.0, scalar2=0.0, op0=ALU.mult, op1=ALU.add,
+                )
 
         def quantise_wv(head):
             if not 0 <= head < H:
@@ -209,7 +210,7 @@ def tile_localselfattention_pa_kernel(tc, q, k_scaled, hidden_states, Wv, out):
                     hs_cols = slice((row_set * HID_PASSES + g) * P, (row_set * HID_PASSES + g + 1) * P)
                     wv_cols = slice((head * HID_PASSES + g) * D, (head * HID_PASSES + g + 1) * D)
                     nc.tensor.matmul_mx(
-                        out=mx_bank[:, row_set, :],
+                        out=project_bank[:, row_set, :],
                         lhsT=hs_codes[chunk][:, hs_cols].bitcast(FP8X4),
                         lhsT_scale=hs_scales[chunk][:, hs_cols],
                         rhs=wv_codes[:, wv_cols].bitcast(FP8X4),
@@ -222,7 +223,7 @@ def tile_localselfattention_pa_kernel(tc, q, k_scaled, hidden_states, Wv, out):
             if not 0 <= group < N_GROUPS:
                 return
             v_grouped[group] = v_grouped_ring.tile([P, D, 4], BF16, name="v_grouped", align_bytes=64)
-            nc.vector.tensor_copy(out=v_grouped[group][:], in_=mx_bank[:].rearrange("p t d -> p d t"))
+            nc.vector.tensor_copy(out=v_grouped[group][:], in_=project_bank[:].rearrange("p t d -> p d t"))
 
         def quantise_v(group):
             if not 0 <= group < N_GROUPS:
@@ -243,13 +244,9 @@ def tile_localselfattention_pa_kernel(tc, q, k_scaled, hidden_states, Wv, out):
             back, own = score_bank[2 * (block % 2)], score_bank[2 * (block % 2) + 1]
             if chunk > 0:
                 nc.tensor.matmul(out=back[:], lhsT=queries, rhs=qk_t[group - H][:, 1, :], start=True, stop=True)
-            if t > 0:
-                nc.tensor.matmul(
-                    out=own[:, 0 : t * P], lhsT=queries, rhs=qk_t[group][:, 1, 0 : t * P], start=True, stop=True
-                )
-            diagonal = slice(t * P, (t + 1) * P)
-            nc.tensor.matmul(out=own[:, diagonal], lhsT=queries, rhs=qk_t[group][:, 1, diagonal], start=True, stop=False)
-            nc.tensor.matmul(out=own[:, diagonal], lhsT=ident_b[:], rhs=mask_b[:], start=False, stop=True)
+            width = (t + 1) * P
+            nc.tensor.matmul(out=own[:, 0:width], lhsT=queries, rhs=qk_t[group][:, 1, 0:width], start=True, stop=False)
+            nc.tensor.matmul(out=own[:, t * P : width], lhsT=ident_b[:], rhs=mask_b[:], start=False, stop=True)
 
         def lift_own(block):
             if not 0 <= block < N_BLOCKS:
@@ -301,7 +298,8 @@ def tile_localselfattention_pa_kernel(tc, q, k_scaled, hidden_states, Wv, out):
                 return
             group, chunk, head, t = place(block)
             words = e_rows[t][:].bitcast(F32)
-            for j in range(2 * first_pass(chunk), 4):
+            last = 3 if t < 2 and block > 0 else 4
+            for j in range(2 * first_pass(chunk), last):
                 nc.tensor.transpose(
                     out=flip_bank[block % 2][:, j, :], in_=words[:, j * P : (j + 1) * P], identity=ident_f[:]
                 )
@@ -334,11 +332,11 @@ def tile_localselfattention_pa_kernel(tc, q, k_scaled, hidden_states, Wv, out):
             if not 0 <= group < N_GROUPS:
                 return
             chunk, head = divmod(group, H)
-            for t in range(QT):
-                block = group * QT + t
+            for n, t in enumerate(BLOCK_ORDER):
+                block = group * QT + n
                 for g in range(first_pass(chunk), 2):
                     nc.tensor.matmul_mx(
-                        out=mx_bank[:, t, :],
+                        out=attend_sums[:, t, :],
                         lhsT=e_codes[block][:, g * P : (g + 1) * P].bitcast(FP8X4),
                         lhsT_scale=e_scales[block][:, g * P : (g + 1) * P],
                         rhs=v_codes[chunk - 1 + g][:, head * D : (head + 1) * D].bitcast(FP8X4),
@@ -353,7 +351,7 @@ def tile_localselfattention_pa_kernel(tc, q, k_scaled, hidden_states, Wv, out):
             out_sb[group] = out_ring.tile([P, QT, D], F32, name="out_sb")
             for t in range(QT):
                 nc.scalar.activation(
-                    out=out_sb[group][:, t, :], in_=mx_bank[:, t, :], func=ACT.Copy, scale=inverse[group][:, t : t + 1]
+                    out=out_sb[group][:, t, :], in_=attend_sums[:, t, :], func=ACT.Copy, scale=inverse[group][:, t : t + 1]
                 )
 
         load_hs(0, 0)
@@ -374,35 +372,41 @@ def tile_localselfattention_pa_kernel(tc, q, k_scaled, hidden_states, Wv, out):
         for t in range(QT - 1):
             nc.vector.memset(e_rows[t][:, CHUNK + (t + 1) * P : 2 * CHUNK], 0.0)
 
-        for tick in range(FIRST_TICK, (N_GROUPS - 1) * QT + LAG + 2):
-            group_now, phase = divmod(tick, QT)
-            lift_own(tick + LIFT_AHEAD)
-            quantise_e(tick - 3)
-            lift_back(tick + LIFT_AHEAD)
-            group_e(tick - 2)
-            exponentials(tick)
-            flip(tick - 1)
-            if phase == 0:
-                attend(group_now - BEHIND)
+        for step in range(FIRST_STEP, (N_GROUPS + BEHIND) * 2):
+            group_now, half = divmod(step, 2)
+            pair = 2 * step
+            for n in range(2):
+                lift_own(pair + 2 + n)
+                quantise_e(pair - 6 + n)
+                lift_back(pair + 2 + n)
+            group_e(pair - 4)
+            group_e(pair - 3)
+            if half == 0:
                 group_hs(hs_job(group_now - 1))
-                group_wv(group_now - BEHIND + 2)
-                quantise_v(group_now - BEHIND + 1)
-            if phase == 1:
+            else:
                 normalise(group_now - BEHIND)
                 store(group_now - BEHIND)
-                transpose_qk(group_now + 2)
+            exponentials(pair)
+            exponentials(pair + 1)
+            flip(pair - 2)
+            flip(pair - 1)
+            if half == 0:
+                attend(group_now - BEHIND)
+                project_v(group_now - BEHIND + 1)
                 quantise_hs(hs_job(group_now - 1))
+                round_v(group_now - BEHIND + 1)
+                group_wv(group_now - BEHIND + 2)
+            else:
+                transpose_qk(group_now + 2)
+                transpose_hs(hs_job(group_now))
+                quantise_v(group_now - BEHIND + 1)
                 quantise_wv(group_now - BEHIND + 2)
+                keep_qk(group_now + 2)
                 invert_sums(group_now - 1)
                 load_qk(group_now + QK_AHEAD)
                 load_wv(group_now + 3)
                 if (group_now + 1) % H == 0:
                     for row_set in range(4):
                         load_hs((group_now + 1) // H + 1, row_set)
-            if phase == 2:
-                project_v(group_now - BEHIND + 2)
-                keep_qk(group_now + 2)
-            if phase == 3:
-                round_v(group_now - BEHIND + 2)
-                transpose_hs(hs_job(group_now))
-            scores(tick + LIFT_AHEAD + 2)
+            scores(pair + 4)
+            scores(pair + 5)

@@ -21,9 +21,8 @@ N_GROUPS = N_CHUNKS * H
 N_BLOCKS = N_GROUPS * QT
 HID_PASSES = HID // K_PASS
 
-BEHIND = 3
 QK_AHEAD = 5
-FIRST_STEP = -5
+CATCH_UP = (6, 7)
 BLOCK_ORDER = (0, 2, 1, 3)
 
 FLOPS = 2 * S * HID * H * D + 2 * (2 * H * D * CHUNK * (CHUNK + (N_CHUNKS - 1) * 2 * CHUNK))
@@ -35,11 +34,23 @@ def place(block):
     return group, chunk, head, BLOCK_ORDER[n]
 
 
-def hs_job(group):
-    chunk, row_set = divmod(group + 3, H)
-    if 0 <= chunk < N_CHUNKS and row_set < 4:
+def hs_job(step):
+    if -2 <= step < 2:
+        return 0, step + 2
+    group, half = divmod(step, 2)
+    chunk, row_set = divmod(group + 6, H)
+    if half == 0 and 1 <= chunk < N_CHUNKS and row_set < 4:
         return chunk, row_set
     return None
+
+
+def v_job(step):
+    group, half = divmod(step, 2)
+    if half == 1:
+        return group - 1 + sum(1 for g in CATCH_UP if g <= group)
+    if group in CATCH_UP:
+        return group - 1 + sum(1 for g in CATCH_UP if g < group)
+    return -1
 
 
 def tile_localselfattention_pa_kernel(tc, q, k_scaled, hidden_states, Wv, out):
@@ -86,9 +97,9 @@ def tile_localselfattention_pa_kernel(tc, q, k_scaled, hidden_states, Wv, out):
         v_grouped_ring = ring("v_grouped", 2)
         lifted_ring = ring("lifted", 6)
         sum_ring = ring("sum", 3)
-        inverse_ring = ring("inverse", BEHIND + 1)
+        inverse_ring = ring("inverse", 4)
         e_grouped_ring = ring("e_grouped", 5)
-        e_mx_ring = ring("e_mx", BEHIND * QT)
+        e_mx_ring = ring("e_mx", 3 * QT)
         out_ring = ring("out", 3)
 
         qk_in, qk_t, hs_in, hs_grouped, hs_codes, hs_scales = {}, {}, {}, {}, {}, {}
@@ -354,12 +365,16 @@ def tile_localselfattention_pa_kernel(tc, q, k_scaled, hidden_states, Wv, out):
                     out=out_sb[group][:, t, :], in_=attend_sums[:, t, :], func=ACT.Copy, scale=inverse[group][:, t : t + 1]
                 )
 
-        load_hs(0, 0)
         load_qk(0)
-        load_hs(0, 1)
+        load_hs(0, 0)
         load_qk(1)
-        load_hs(0, 2)
-        load_hs(0, 3)
+        for row_set in range(1, 4):
+            load_hs(0, row_set)
+        load_wv(0)
+        load_qk(2)
+        load_qk(3)
+        load_wv(1)
+        load_qk(4)
 
         make_identity(nc, ident_f[:])
         make_identity(nc, ident_b[:])
@@ -372,7 +387,23 @@ def tile_localselfattention_pa_kernel(tc, q, k_scaled, hidden_states, Wv, out):
         for t in range(QT - 1):
             nc.vector.memset(e_rows[t][:, CHUNK + (t + 1) * P : 2 * CHUNK], 0.0)
 
-        for step in range(FIRST_STEP, (N_GROUPS + BEHIND) * 2):
+        transpose_qk(0)
+        keep_qk(0)
+        transpose_hs(hs_job(-2))
+        group_hs(hs_job(-2))
+        for block in range(2):
+            scores(block)
+        for block in range(2):
+            lift_own(block)
+            lift_back(block)
+        transpose_qk(1)
+        keep_qk(1)
+        quantise_hs(hs_job(-2))
+        for block in range(2, 4):
+            scores(block)
+        transpose_hs(hs_job(-1))
+
+        for step in range(2 * N_GROUPS + 5):
             group_now, half = divmod(step, 2)
             pair = 2 * step
             for n in range(2):
@@ -381,32 +412,32 @@ def tile_localselfattention_pa_kernel(tc, q, k_scaled, hidden_states, Wv, out):
                 lift_back(pair + 2 + n)
             group_e(pair - 4)
             group_e(pair - 3)
+            group_hs(hs_job(step - 1))
             if half == 0:
-                group_hs(hs_job(group_now - 1))
-            else:
-                normalise(group_now - BEHIND)
-                store(group_now - BEHIND)
+                normalise(group_now - 3)
+                store(group_now - 3)
             exponentials(pair)
             exponentials(pair + 1)
             flip(pair - 2)
             flip(pair - 1)
             if half == 0:
-                attend(group_now - BEHIND)
-                project_v(group_now - BEHIND + 1)
-                quantise_hs(hs_job(group_now - 1))
-                round_v(group_now - BEHIND + 1)
-                group_wv(group_now - BEHIND + 2)
-            else:
                 transpose_qk(group_now + 2)
-                transpose_hs(hs_job(group_now))
-                quantise_v(group_now - BEHIND + 1)
-                quantise_wv(group_now - BEHIND + 2)
+            else:
+                attend(group_now - 2)
+            transpose_hs(hs_job(step))
+            project_v(v_job(step))
+            quantise_v(v_job(step - 1))
+            quantise_hs(hs_job(step - 1))
+            quantise_wv(step - 2)
+            group_wv(step - 1)
+            if half == 0:
                 keep_qk(group_now + 2)
-                invert_sums(group_now - 1)
                 load_qk(group_now + QK_AHEAD)
-                load_wv(group_now + 3)
-                if (group_now + 1) % H == 0:
+                if group_now % H == 0:
                     for row_set in range(4):
-                        load_hs((group_now + 1) // H + 1, row_set)
+                        load_hs(group_now // H + 1, row_set)
+            else:
+                invert_sums(group_now - 1)
+            round_v(v_job(step))
             scores(pair + 4)
             scores(pair + 5)

@@ -23,7 +23,7 @@ HID_PASSES = HID // K_PASS
 
 QK_AHEAD = 5
 CATCH_UP = (6, 7)
-BLOCK_ORDER = (0, 2, 1, 3)
+BLOCK_ORDER = (0, 3, 1, 2)
 
 FLOPS = 2 * S * HID * H * D + 2 * (2 * H * D * CHUNK * (CHUNK + (N_CHUNKS - 1) * 2 * CHUNK))
 
@@ -71,10 +71,11 @@ def tile_localselfattention_pa_kernel(tc, q, k_scaled, hidden_states, Wv, out):
 
         score_bank = [banks.tile([P, CHUNK], F32, name="score_bank%d" % n) for n in range(4)]
         flip_bank = [banks.tile([P, 4, P], F32, name="flip_bank%d" % n) for n in range(2)]
-        attend_bank = banks.tile([P, 4 * P], F32, name="attend_bank")
-        attend_sums = attend_bank[:].rearrange("p (t d) -> p t d", d=D)
-        attend_halves = attend_bank[:].bitcast(BF16)
-        project_bank = banks.tile([P, 4, P], F32, name="project_bank")
+        side_bank = [banks.tile([P, 4 * P], F32, name="side_bank%d" % n) for n in range(2)]
+
+        def pieces(bank):
+            return bank[:].rearrange("p (j r) -> p j r", r=P)
+
 
         ident_f = fixed.tile([P, P], F32, name="ident_f")
         ident_b = fixed.tile([P, P], BF16, name="ident_b")
@@ -146,37 +147,37 @@ def tile_localselfattention_pa_kernel(tc, q, k_scaled, hidden_states, Wv, out):
                 in_=out_sb[group][:],
             )
 
-        def transpose_qk(group):
+        def transpose_qk(group, bank):
             if not 0 <= group < N_GROUPS:
                 return
             for a in range(2):
                 for t in range(QT):
                     n = a * QT + t
                     nc.tensor.transpose(
-                        out=attend_halves[:, n * P : (n + 1) * P], in_=qk_in[group][:, a, t, :], identity=ident_b[:]
+                        out=bank[:].bitcast(BF16)[:, n * P : (n + 1) * P], in_=qk_in[group][:, a, t, :], identity=ident_b[:]
                     )
 
-        def keep_qk(group):
+        def keep_qk(group, bank, copy):
             if not 0 <= group < N_GROUPS:
                 return
             qk_t[group] = qk_t_ring.tile([P, 2, CHUNK], BF16, name="qk_t")
-            nc.vector.tensor_copy(out=qk_t[group][:], in_=attend_halves.rearrange("p (a s) -> p a s", a=2))
+            copy(out=qk_t[group][:], in_=bank[:].bitcast(BF16).rearrange("p (a s) -> p a s", a=2))
 
-        def transpose_hs(job):
+        def transpose_hs(job, bank):
             if job is None:
                 return
             chunk, row_set = job
             words = hs_in[chunk][:, row_set, :].bitcast(F32)
             for j in range(4):
-                nc.tensor.transpose(out=project_bank[:, j, :], in_=words[:, j * P : (j + 1) * P], identity=ident_f[:])
+                nc.tensor.transpose(out=pieces(bank)[:, j, :], in_=words[:, j * P : (j + 1) * P], identity=ident_f[:])
 
-        def group_hs(job):
+        def group_hs(job, bank):
             if job is None:
                 return
             hs_grouped[job] = hs_grouped_ring.tile([P, HID_PASSES * K_PASS], BF16, name="hs_grouped", align_bytes=64)
             nc.scalar.copy(
                 out=hs_grouped[job][:].bitcast(F32).rearrange("p (g r u) -> p g r u", r=P, u=2),
-                in_=project_bank[:].rearrange("p (g u) r -> p g r u", u=2),
+                in_=pieces(bank).rearrange("p (g u) r -> p g r u", u=2),
             )
 
         def quantise_hs(job):
@@ -221,7 +222,7 @@ def tile_localselfattention_pa_kernel(tc, q, k_scaled, hidden_states, Wv, out):
                     hs_cols = slice((row_set * HID_PASSES + g) * P, (row_set * HID_PASSES + g + 1) * P)
                     wv_cols = slice((head * HID_PASSES + g) * D, (head * HID_PASSES + g + 1) * D)
                     nc.tensor.matmul_mx(
-                        out=project_bank[:, row_set, :],
+                        out=pieces(side_bank[1])[:, row_set, :],
                         lhsT=hs_codes[chunk][:, hs_cols].bitcast(FP8X4),
                         lhsT_scale=hs_scales[chunk][:, hs_cols],
                         rhs=wv_codes[:, wv_cols].bitcast(FP8X4),
@@ -230,11 +231,11 @@ def tile_localselfattention_pa_kernel(tc, q, k_scaled, hidden_states, Wv, out):
                         stop=(g == HID_PASSES - 1),
                     )
 
-        def round_v(group):
+        def round_v(group, copy):
             if not 0 <= group < N_GROUPS:
                 return
             v_grouped[group] = v_grouped_ring.tile([P, D, 4], BF16, name="v_grouped", align_bytes=64)
-            nc.vector.tensor_copy(out=v_grouped[group][:], in_=project_bank[:].rearrange("p t d -> p d t"))
+            copy(out=v_grouped[group][:], in_=pieces(side_bank[1]).rearrange("p t d -> p d t"))
 
         def quantise_v(group):
             if not 0 <= group < N_GROUPS:
@@ -315,13 +316,13 @@ def tile_localselfattention_pa_kernel(tc, q, k_scaled, hidden_states, Wv, out):
                     out=flip_bank[block % 2][:, j, :], in_=words[:, j * P : (j + 1) * P], identity=ident_f[:]
                 )
 
-        def group_e(block):
+        def group_e(block, copy):
             if not 0 <= block < N_BLOCKS:
                 return
             group, chunk, head, t = place(block)
             g0 = first_pass(chunk)
             e_grouped[block] = e_grouped_ring.tile([P, 2 * K_PASS], BF16, name="e_grouped", align_bytes=64)
-            nc.scalar.copy(
+            copy(
                 out=e_grouped[block][:].bitcast(F32)[:, g0 * 2 * P : 4 * P].rearrange("p (g r u) -> p g r u", r=P, u=2),
                 in_=flip_bank[block % 2][:, 2 * g0 : 4, :].rearrange("p (g u) r -> p g r u", u=2),
             )
@@ -339,7 +340,7 @@ def tile_localselfattention_pa_kernel(tc, q, k_scaled, hidden_states, Wv, out):
                 in_=e_grouped[block][:, g0 * K_PASS : 2 * K_PASS],
             )
 
-        def attend(group):
+        def attend(group, bank):
             if not 0 <= group < N_GROUPS:
                 return
             chunk, head = divmod(group, H)
@@ -347,7 +348,7 @@ def tile_localselfattention_pa_kernel(tc, q, k_scaled, hidden_states, Wv, out):
                 block = group * QT + n
                 for g in range(first_pass(chunk), 2):
                     nc.tensor.matmul_mx(
-                        out=attend_sums[:, t, :],
+                        out=pieces(bank)[:, t, :],
                         lhsT=e_codes[block][:, g * P : (g + 1) * P].bitcast(FP8X4),
                         lhsT_scale=e_scales[block][:, g * P : (g + 1) * P],
                         rhs=v_codes[chunk - 1 + g][:, head * D : (head + 1) * D].bitcast(FP8X4),
@@ -356,22 +357,23 @@ def tile_localselfattention_pa_kernel(tc, q, k_scaled, hidden_states, Wv, out):
                         stop=(g == 1),
                     )
 
-        def normalise(group):
+        def normalise(group, bank):
             if not 0 <= group < N_GROUPS:
                 return
             out_sb[group] = out_ring.tile([P, QT, D], F32, name="out_sb")
-            for t in range(QT):
-                nc.scalar.activation(
-                    out=out_sb[group][:, t, :], in_=attend_sums[:, t, :], func=ACT.Copy, scale=inverse[group][:, t : t + 1]
-                )
+            nc.vector.tensor_tensor(
+                out=out_sb[group][:], in0=pieces(bank), in1=inverse[group][:].unsqueeze(2).to_broadcast([P, QT, D]),
+                op=ALU.mult,
+            )
 
         load_qk(0)
-        load_hs(0, 0)
         load_qk(1)
-        for row_set in range(1, 4):
-            load_hs(0, row_set)
-        load_wv(0)
+        load_hs(0, 0)
+        load_hs(0, 1)
         load_qk(2)
+        load_hs(0, 2)
+        load_hs(0, 3)
+        load_wv(0)
         load_qk(3)
         load_wv(1)
         load_qk(4)
@@ -387,57 +389,106 @@ def tile_localselfattention_pa_kernel(tc, q, k_scaled, hidden_states, Wv, out):
         for t in range(QT - 1):
             nc.vector.memset(e_rows[t][:, CHUNK + (t + 1) * P : 2 * CHUNK], 0.0)
 
-        transpose_qk(0)
-        keep_qk(0)
-        transpose_hs(hs_job(-2))
-        group_hs(hs_job(-2))
+        transpose_qk(0, side_bank[0])
+        keep_qk(0, side_bank[0], nc.scalar.copy)
+        transpose_qk(1, side_bank[1])
+        keep_qk(1, side_bank[1], nc.vector.tensor_copy)
         for block in range(2):
             scores(block)
         for block in range(2):
             lift_own(block)
             lift_back(block)
-        transpose_qk(1)
-        keep_qk(1)
-        quantise_hs(hs_job(-2))
+        transpose_hs(hs_job(-2), side_bank[0])
         for block in range(2, 4):
             scores(block)
-        transpose_hs(hs_job(-1))
+        transpose_hs(hs_job(-1), side_bank[1])
 
-        for step in range(2 * N_GROUPS + 5):
+        for step in range(2 * N_GROUPS - 1):
             group_now, half = divmod(step, 2)
             pair = 2 * step
-            for n in range(2):
-                lift_own(pair + 2 + n)
-                quantise_e(pair - 6 + n)
-                lift_back(pair + 2 + n)
-            group_e(pair - 4)
-            group_e(pair - 3)
-            group_hs(hs_job(step - 1))
-            if half == 0:
-                normalise(group_now - 3)
-                store(group_now - 3)
+            lift_own(pair + 2)
+            quantise_e(pair - 6)
+            lift_back(pair + 2)
+            if v_job(step - 1) % 2 == 0:
+                round_v(v_job(step - 1), nc.vector.tensor_copy)
+            lift_own(pair + 3)
+            quantise_e(pair - 5)
+            lift_back(pair + 3)
+            group_e(pair - 4, nc.scalar.copy)
+            group_e(pair - 3, nc.scalar.copy)
+            if half == 1:
+                keep_qk(group_now + 2, side_bank[0], nc.scalar.copy)
+            if step > 2:
+                group_hs(hs_job(step - 1), side_bank[1])
             exponentials(pair)
+            if v_job(step - 1) % 2 == 1:
+                round_v(v_job(step - 1), nc.scalar.copy)
             exponentials(pair + 1)
-            flip(pair - 2)
-            flip(pair - 1)
+            if step == 0:
+                group_hs(hs_job(-2), side_bank[0])
+                quantise_hs(hs_job(-2))
+            if step <= 2:
+                group_hs(hs_job(step - 1), side_bank[1])
             if half == 0:
-                transpose_qk(group_now + 2)
+                flip(pair - 2)
+                flip(pair - 1)
+                transpose_qk(group_now + 2, side_bank[0])
+                scores(pair + 4)
+                transpose_hs(hs_job(step), side_bank[1])
+                project_v(v_job(step))
+                scores(pair + 5)
             else:
-                attend(group_now - 2)
-            transpose_hs(hs_job(step))
-            project_v(v_job(step))
-            quantise_v(v_job(step - 1))
+                flip(pair - 2)
+                flip(pair - 1)
+                attend(group_now - 2, side_bank[0])
+                scores(pair + 4)
+                transpose_hs(hs_job(step), side_bank[1])
+                project_v(v_job(step))
+                scores(pair + 5)
             quantise_hs(hs_job(step - 1))
             quantise_wv(step - 2)
             group_wv(step - 1)
             if half == 0:
-                keep_qk(group_now + 2)
                 load_qk(group_now + QK_AHEAD)
                 if group_now % H == 0:
                     for row_set in range(4):
                         load_hs(group_now // H + 1, row_set)
             else:
                 invert_sums(group_now - 1)
-            round_v(v_job(step))
-            scores(pair + 4)
-            scores(pair + 5)
+                normalise(group_now - 2, side_bank[0])
+                store(group_now - 2)
+            quantise_v(v_job(step - 1))
+
+        last = N_BLOCKS - 1
+        group = N_GROUPS - 1
+        quantise_e(last - 7)
+        quantise_e(last - 6)
+        group_e(last - 5, nc.scalar.copy)
+        group_e(last - 4, nc.vector.tensor_copy)
+        exponentials(last - 1)
+        exponentials(last)
+        attend(group - 2, side_bank[0])
+        flip(last - 3)
+        flip(last - 2)
+        normalise(group - 2, side_bank[0])
+        store(group - 2)
+        quantise_e(last - 5)
+        quantise_e(last - 4)
+        attend(group - 1, side_bank[0])
+        group_e(last - 3, nc.scalar.copy)
+        group_e(last - 2, nc.scalar.copy)
+        flip(last - 1)
+        flip(last)
+        invert_sums(group - 1)
+        quantise_e(last - 3)
+        quantise_e(last - 2)
+        normalise(group - 1, side_bank[0])
+        store(group - 1)
+        group_e(last - 1, nc.scalar.copy)
+        group_e(last, nc.vector.tensor_copy)
+        quantise_e(last - 1)
+        invert_sums(group)
+        quantise_e(last)
+        attend(group, side_bank[1])
+        normalise(group, side_bank[1])
+        store(group)

@@ -22,7 +22,7 @@ N_BLOCKS = N_GROUPS * QT
 HID_PASSES = HID // K_PASS
 
 QK_AHEAD = 5
-CATCH_UP = (6, 7)
+CATCH_UP = (25, 27)
 BLOCK_ORDER = (0, 3, 1, 2)
 
 FLOPS = 2 * S * HID * H * D + 2 * (2 * H * D * CHUNK * (CHUNK + (N_CHUNKS - 1) * 2 * CHUNK))
@@ -38,7 +38,7 @@ def hs_job(step):
     if -2 <= step < 2:
         return 0, step + 2
     group, half = divmod(step, 2)
-    chunk, row_set = divmod(group + 6, H)
+    chunk, row_set = divmod(group + 3, H)
     if half == 0 and 1 <= chunk < N_CHUNKS and row_set < 4:
         return chunk, row_set
     return None
@@ -70,7 +70,7 @@ def tile_localselfattention_pa_kernel(tc, q, k_scaled, hidden_states, Wv, out):
         banks = stack.enter_context(tc.psum_pool(name="banks", bufs=1))
 
         score_bank = [banks.tile([P, CHUNK], F32, name="score_bank%d" % n) for n in range(4)]
-        flip_bank = [banks.tile([P, 4, P], F32, name="flip_bank%d" % n) for n in range(2)]
+        flip_bank = [banks.tile([P, 4 * P], F32, name="flip_bank%d" % n) for n in range(2)]
         side_bank = [banks.tile([P, 4 * P], F32, name="side_bank%d" % n) for n in range(2)]
 
         def pieces(bank):
@@ -81,6 +81,7 @@ def tile_localselfattention_pa_kernel(tc, q, k_scaled, hidden_states, Wv, out):
         ident_b = fixed.tile([P, P], BF16, name="ident_b")
         mask_f = fixed.tile([P, P], F32, name="mask_f")
         mask_b = fixed.tile([P, P], BF16, name="mask_b")
+        minus_one = fixed.tile([P, QT], F32, name="minus_one")
         e_rows = [fixed.tile([P, 2 * CHUNK], BF16, name="e_rows%d" % t) for t in range(QT)]
 
         wv_in = fixed.tile([P, HID_PASSES, 4, H * D], BF16, name="wv_in")
@@ -300,20 +301,23 @@ def tile_localselfattention_pa_kernel(tc, q, k_scaled, hidden_states, Wv, out):
             if not 0 <= group < N_GROUPS:
                 return
             inverse[group] = inverse_ring.tile([P, QT], F32, name="inverse")
-            nc.vector.reciprocal(out=inverse[group][:], in_=row_sum[group][:])
+            nc.gpsimd.tensor_tensor(out=inverse[group][:], in0=row_sum[group][:], in1=minus_one[:], op=ALU.pow)
 
         def first_pass(chunk):
             return 0 if chunk > 0 else 1
+
+        def flip_to(block):
+            return flip_bank[block % 2] if block < N_BLOCKS - 2 else score_bank[block % 2]
 
         def flip(block):
             if not 0 <= block < N_BLOCKS:
                 return
             group, chunk, head, t = place(block)
             words = e_rows[t][:].bitcast(F32)
-            last = 3 if t < 2 and block > 0 else 4
+            last = 3 if t < 2 and 0 < block < N_BLOCKS - 2 else 4
             for j in range(2 * first_pass(chunk), last):
                 nc.tensor.transpose(
-                    out=flip_bank[block % 2][:, j, :], in_=words[:, j * P : (j + 1) * P], identity=ident_f[:]
+                    out=pieces(flip_to(block))[:, j, :], in_=words[:, j * P : (j + 1) * P], identity=ident_f[:]
                 )
 
         def group_e(block, copy):
@@ -324,7 +328,7 @@ def tile_localselfattention_pa_kernel(tc, q, k_scaled, hidden_states, Wv, out):
             e_grouped[block] = e_grouped_ring.tile([P, 2 * K_PASS], BF16, name="e_grouped", align_bytes=64)
             copy(
                 out=e_grouped[block][:].bitcast(F32)[:, g0 * 2 * P : 4 * P].rearrange("p (g r u) -> p g r u", r=P, u=2),
-                in_=flip_bank[block % 2][:, 2 * g0 : 4, :].rearrange("p (g u) r -> p g r u", u=2),
+                in_=pieces(flip_to(block))[:, 2 * g0 : 4, :].rearrange("p (g u) r -> p g r u", u=2),
             )
 
         def quantise_e(block):
@@ -340,11 +344,12 @@ def tile_localselfattention_pa_kernel(tc, q, k_scaled, hidden_states, Wv, out):
                 in_=e_grouped[block][:, g0 * K_PASS : 2 * K_PASS],
             )
 
-        def attend(group, bank):
+        def attend(group, bank, part=range(QT)):
             if not 0 <= group < N_GROUPS:
                 return
             chunk, head = divmod(group, H)
-            for n, t in enumerate(BLOCK_ORDER):
+            for n in part:
+                t = BLOCK_ORDER[n]
                 block = group * QT + n
                 for g in range(first_pass(chunk), 2):
                     nc.tensor.matmul_mx(
@@ -357,14 +362,23 @@ def tile_localselfattention_pa_kernel(tc, q, k_scaled, hidden_states, Wv, out):
                         stop=(g == 1),
                     )
 
-        def normalise(group, bank):
+        def normalise(group, bank, first=0, end=QT):
             if not 0 <= group < N_GROUPS:
                 return
-            out_sb[group] = out_ring.tile([P, QT, D], F32, name="out_sb")
+            if group not in out_sb:
+                out_sb[group] = out_ring.tile([P, QT, D], F32, name="out_sb")
             nc.vector.tensor_tensor(
-                out=out_sb[group][:], in0=pieces(bank), in1=inverse[group][:].unsqueeze(2).to_broadcast([P, QT, D]),
-                op=ALU.mult,
+                out=out_sb[group][:, first:end, :], in0=pieces(bank)[:, first:end, :],
+                in1=inverse[group][:, first:end].unsqueeze(2).to_broadcast([P, end - first, D]), op=ALU.mult,
             )
+
+        def normalise_on_scalar(group, bank, tiles=range(QT)):
+            if group not in out_sb:
+                out_sb[group] = out_ring.tile([P, QT, D], F32, name="out_sb")
+            for t in tiles:
+                nc.scalar.activation(
+                    out=out_sb[group][:, t, :], in_=pieces(bank)[:, t, :], func=ACT.Copy, scale=inverse[group][:, t : t + 1]
+                )
 
         load_qk(0)
         load_qk(1)
@@ -386,8 +400,12 @@ def tile_localselfattention_pa_kernel(tc, q, k_scaled, hidden_states, Wv, out):
             channel_multiplier=1,
         )
         nc.vector.tensor_copy(out=mask_b[:], in_=mask_f[:])
+        nc.gpsimd.memset(minus_one[:], -1.0)
         for t in range(QT - 1):
             nc.vector.memset(e_rows[t][:, CHUNK + (t + 1) * P : 2 * CHUNK], 0.0)
+
+        def qk_bank(group):
+            return score_bank[0] if group < H else side_bank[0]
 
         transpose_qk(0, side_bank[0])
         keep_qk(0, side_bank[0], nc.scalar.copy)
@@ -409,7 +427,7 @@ def tile_localselfattention_pa_kernel(tc, q, k_scaled, hidden_states, Wv, out):
             lift_own(pair + 2)
             quantise_e(pair - 6)
             lift_back(pair + 2)
-            if v_job(step - 1) % 2 == 0:
+            if (v_job(step - 1) % 2 == 0 and v_job(step - 1) >= H):
                 round_v(v_job(step - 1), nc.vector.tensor_copy)
             lift_own(pair + 3)
             quantise_e(pair - 5)
@@ -417,11 +435,11 @@ def tile_localselfattention_pa_kernel(tc, q, k_scaled, hidden_states, Wv, out):
             group_e(pair - 4, nc.scalar.copy)
             group_e(pair - 3, nc.scalar.copy)
             if half == 1:
-                keep_qk(group_now + 2, side_bank[0], nc.scalar.copy)
+                keep_qk(group_now + 2, qk_bank(group_now + 2), nc.scalar.copy)
             if step > 2:
                 group_hs(hs_job(step - 1), side_bank[1])
             exponentials(pair)
-            if v_job(step - 1) % 2 == 1:
+            if (v_job(step - 1) % 2 == 1 or v_job(step - 1) < H):
                 round_v(v_job(step - 1), nc.scalar.copy)
             exponentials(pair + 1)
             if step == 0:
@@ -432,7 +450,7 @@ def tile_localselfattention_pa_kernel(tc, q, k_scaled, hidden_states, Wv, out):
             if half == 0:
                 flip(pair - 2)
                 flip(pair - 1)
-                transpose_qk(group_now + 2, side_bank[0])
+                transpose_qk(group_now + 2, qk_bank(group_now + 2))
                 scores(pair + 4)
                 transpose_hs(hs_job(step), side_bank[1])
                 project_v(v_job(step))
@@ -445,16 +463,17 @@ def tile_localselfattention_pa_kernel(tc, q, k_scaled, hidden_states, Wv, out):
                 transpose_hs(hs_job(step), side_bank[1])
                 project_v(v_job(step))
                 scores(pair + 5)
-            quantise_hs(hs_job(step - 1))
-            quantise_wv(step - 2)
             group_wv(step - 1)
             if half == 0:
                 load_qk(group_now + QK_AHEAD)
                 if group_now % H == 0:
                     for row_set in range(4):
                         load_hs(group_now // H + 1, row_set)
-            else:
+            quantise_hs(hs_job(step - 1))
+            quantise_wv(step - 2)
+            if half == 1:
                 invert_sums(group_now - 1)
+            if half == 1:
                 normalise(group_now - 2, side_bank[0])
                 store(group_now - 2)
             quantise_v(v_job(step - 1))
@@ -467,28 +486,30 @@ def tile_localselfattention_pa_kernel(tc, q, k_scaled, hidden_states, Wv, out):
         group_e(last - 4, nc.vector.tensor_copy)
         exponentials(last - 1)
         exponentials(last)
+        invert_sums(group - 1)
+        invert_sums(group)
         attend(group - 2, side_bank[0])
         flip(last - 3)
         flip(last - 2)
-        normalise(group - 2, side_bank[0])
-        store(group - 2)
         quantise_e(last - 5)
         quantise_e(last - 4)
-        attend(group - 1, side_bank[0])
         group_e(last - 3, nc.scalar.copy)
-        group_e(last - 2, nc.scalar.copy)
+        group_e(last - 2, nc.vector.tensor_copy)
         flip(last - 1)
         flip(last)
-        invert_sums(group - 1)
+        attend(group - 1, side_bank[1])
         quantise_e(last - 3)
         quantise_e(last - 2)
-        normalise(group - 1, side_bank[0])
-        store(group - 1)
         group_e(last - 1, nc.scalar.copy)
         group_e(last, nc.vector.tensor_copy)
+        attend(group, score_bank[2], (0, 1))
+        normalise_on_scalar(group - 2, side_bank[0])
+        store(group - 2)
+        normalise_on_scalar(group - 1, side_bank[1])
+        store(group - 1)
         quantise_e(last - 1)
-        invert_sums(group)
         quantise_e(last)
-        attend(group, side_bank[1])
-        normalise(group, side_bank[1])
+        attend(group, score_bank[3], (2, 3))
+        normalise_on_scalar(group, score_bank[2], (0, 3))
+        normalise(group, score_bank[3], 1, 3)
         store(group)

@@ -81,7 +81,6 @@ def tile_localselfattention_pa_kernel(tc, q, k_scaled, hidden_states, Wv, out):
         ident_b = fixed.tile([P, P], BF16, name="ident_b")
         mask_f = fixed.tile([P, P], F32, name="mask_f")
         mask_b = fixed.tile([P, P], BF16, name="mask_b")
-        minus_one = fixed.tile([P, QT], F32, name="minus_one")
         e_rows = [fixed.tile([P, 2 * CHUNK], BF16, name="e_rows%d" % t) for t in range(QT)]
 
         wv_in = fixed.tile([P, HID_PASSES, 4, H * D], BF16, name="wv_in")
@@ -301,7 +300,7 @@ def tile_localselfattention_pa_kernel(tc, q, k_scaled, hidden_states, Wv, out):
             if not 0 <= group < N_GROUPS:
                 return
             inverse[group] = inverse_ring.tile([P, QT], F32, name="inverse")
-            nc.gpsimd.tensor_tensor(out=inverse[group][:], in0=row_sum[group][:], in1=minus_one[:], op=ALU.pow)
+            nc.vector.reciprocal(out=inverse[group][:], in_=row_sum[group][:])
 
         def first_pass(chunk):
             return 0 if chunk > 0 else 1
@@ -400,7 +399,6 @@ def tile_localselfattention_pa_kernel(tc, q, k_scaled, hidden_states, Wv, out):
             channel_multiplier=1,
         )
         nc.vector.tensor_copy(out=mask_b[:], in_=mask_f[:])
-        nc.gpsimd.memset(minus_one[:], -1.0)
         for t in range(QT - 1):
             nc.vector.memset(e_rows[t][:, CHUNK + (t + 1) * P : 2 * CHUNK], 0.0)
 

@@ -96,12 +96,12 @@ def tile_localselfattention_pa_kernel(tc, q, k_scaled, hidden_states, Wv, out):
         hs_mx_ring = ring("hs_mx", 2)
         wv_grouped_ring = ring("wv_grouped", 2)
         v_grouped_ring = ring("v_grouped", 2)
-        lifted_ring = ring("lifted", 6)
+        lifted_ring = ring("lifted", 8)
         sum_ring = ring("sum", 3)
         inverse_ring = ring("inverse", 4)
-        e_grouped_ring = ring("e_grouped", 5)
+        e_grouped_ring = ring("e_grouped", 8)
         e_mx_ring = ring("e_mx", 3 * QT)
-        out_ring = ring("out", 3)
+        out_ring = ring("out", 20)
 
         qk_in, qk_t, hs_in, hs_grouped, hs_codes, hs_scales = {}, {}, {}, {}, {}, {}
         wv_grouped, v_grouped, lifted, neg_own, neg_top, row_sum, inverse = {}, {}, {}, {}, {}, {}, {}

@@ -254,11 +254,11 @@ def tile_localselfattention_pa_kernel(tc, q, k_scaled, hidden_states, Wv, out):
             group, chunk, head, t = place(block)
             queries = qk_t[group][:, 0, t * P : (t + 1) * P]
             back, own = score_bank[2 * (block % 2)], score_bank[2 * (block % 2) + 1]
-            if chunk > 0:
-                nc.tensor.matmul(out=back[:], lhsT=queries, rhs=qk_t[group - H][:, 1, :], start=True, stop=True)
             width = (t + 1) * P
             nc.tensor.matmul(out=own[:, 0:width], lhsT=queries, rhs=qk_t[group][:, 1, 0:width], start=True, stop=False)
             nc.tensor.matmul(out=own[:, t * P : width], lhsT=ident_b[:], rhs=mask_b[:], start=False, stop=True)
+            if chunk > 0:
+                nc.tensor.matmul(out=back[:], lhsT=queries, rhs=qk_t[group - H][:, 1, :], start=True, stop=True)
 
         def lift_own(block):
             if not 0 <= block < N_BLOCKS:
@@ -461,14 +461,16 @@ def tile_localselfattention_pa_kernel(tc, q, k_scaled, hidden_states, Wv, out):
                 transpose_hs(hs_job(step), side_bank[1])
                 project_v(v_job(step))
                 scores(pair + 5)
-            group_wv(step - 1)
+            if half == 1:
+                group_wv(group_now)
             if half == 0:
                 load_qk(group_now + QK_AHEAD)
                 if group_now % H == 0:
                     for row_set in range(4):
                         load_hs(group_now // H + 1, row_set)
             quantise_hs(hs_job(step - 1))
-            quantise_wv(step - 2)
+            if half == 0:
+                quantise_wv(group_now - 1)
             if half == 1:
                 invert_sums(group_now - 1)
             if half == 1:

@@ -96,12 +96,12 @@ def tile_localselfattention_pa_kernel(tc, q, k_scaled, hidden_states, Wv, out):
         hs_mx_ring = ring("hs_mx", 2)
         wv_grouped_ring = ring("wv_grouped", 2)
         v_grouped_ring = ring("v_grouped", 2)
-        lifted_ring = ring("lifted", 8)
+        lifted_ring = ring("lifted", 6)
         sum_ring = ring("sum", 3)
         inverse_ring = ring("inverse", 4)
-        e_grouped_ring = ring("e_grouped", 8)
+        e_grouped_ring = ring("e_grouped", 7)
         e_mx_ring = ring("e_mx", 3 * QT)
-        out_ring = ring("out", 20)
+        out_ring = ring("out", 26)
 
         qk_in, qk_t, hs_in, hs_grouped, hs_codes, hs_scales = {}, {}, {}, {}, {}, {}
         wv_grouped, v_grouped, lifted, neg_own, neg_top, row_sum, inverse = {}, {}, {}, {}, {}, {}, {}
@@ -288,19 +288,20 @@ def tile_localselfattention_pa_kernel(tc, q, k_scaled, hidden_states, Wv, out):
             if not 0 <= block < N_BLOCKS:
                 return
             group, chunk, head, t = place(block)
-            if t == 0:
-                row_sum[group] = sum_ring.tile([P, QT], F32, name="row_sum")
+            if block % (2 * QT) == 0:
+                row_sum[group // 2] = sum_ring.tile([P, 2 * QT], F32, name="row_sum")
             keys = slice(0 if chunk > 0 else CHUNK, CHUNK + (t + 1) * P)
+            column = group % 2 * QT + t
             nc.scalar.activation(
                 out=e_rows[t][:, keys], in_=lifted[block][:, keys], func=ACT.Exp,
-                bias=neg_top[block][:], scale=-1.0, accum_out=row_sum[group][:, t : t + 1],
+                bias=neg_top[block][:], scale=-1.0, accum_out=row_sum[group // 2][:, column : column + 1],
             )
 
-        def invert_sums(group):
-            if not 0 <= group < N_GROUPS:
+        def invert_sums(group_pair):
+            if not 0 <= group_pair < N_GROUPS // 2:
                 return
-            inverse[group] = inverse_ring.tile([P, QT], F32, name="inverse")
-            nc.vector.reciprocal(out=inverse[group][:], in_=row_sum[group][:])
+            inverse[group_pair] = inverse_ring.tile([P, 2 * QT], F32, name="inverse")
+            nc.vector.reciprocal(out=inverse[group_pair][:], in_=row_sum[group_pair][:])
 
         def first_pass(chunk):
             return 0 if chunk > 0 else 1
@@ -368,7 +369,7 @@ def tile_localselfattention_pa_kernel(tc, q, k_scaled, hidden_states, Wv, out):
                 out_sb[group] = out_ring.tile([P, QT, D], F32, name="out_sb")
             nc.vector.tensor_tensor(
                 out=out_sb[group][:, first:end, :], in0=pieces(bank)[:, first:end, :],
-                in1=inverse[group][:, first:end].unsqueeze(2).to_broadcast([P, end - first, D]), op=ALU.mult,
+                in1=inverse[group // 2][:, group % 2 * QT + first : group % 2 * QT + end].unsqueeze(2).to_broadcast([P, end - first, D]), op=ALU.mult,
             )
 
         def normalise_on_scalar(group, bank, tiles=range(QT)):
@@ -376,7 +377,7 @@ def tile_localselfattention_pa_kernel(tc, q, k_scaled, hidden_states, Wv, out):
                 out_sb[group] = out_ring.tile([P, QT, D], F32, name="out_sb")
             for t in tiles:
                 nc.scalar.activation(
-                    out=out_sb[group][:, t, :], in_=pieces(bank)[:, t, :], func=ACT.Copy, scale=inverse[group][:, t : t + 1]
+                    out=out_sb[group][:, t, :], in_=pieces(bank)[:, t, :], func=ACT.Copy, scale=inverse[group // 2][:, group % 2 * QT + t : group % 2 * QT + t + 1]
                 )
 
         load_qk(0)
@@ -437,9 +438,9 @@ def tile_localselfattention_pa_kernel(tc, q, k_scaled, hidden_states, Wv, out):
             if step > 2:
                 group_hs(hs_job(step - 1), side_bank[1])
             exponentials(pair)
+            exponentials(pair + 1)
             if (v_job(step - 1) % 2 == 1 or v_job(step - 1) < H):
                 round_v(v_job(step - 1), nc.scalar.copy)
-            exponentials(pair + 1)
             if step == 0:
                 group_hs(hs_job(-2), side_bank[0])
                 quantise_hs(hs_job(-2))
@@ -471,8 +472,8 @@ def tile_localselfattention_pa_kernel(tc, q, k_scaled, hidden_states, Wv, out):
             quantise_hs(hs_job(step - 1))
             if half == 0:
                 quantise_wv(group_now - 1)
-            if half == 1:
-                invert_sums(group_now - 1)
+            if half == 0 and group_now % 2 == 0:
+                invert_sums(group_now // 2 - 1)
             if half == 1:
                 normalise(group_now - 2, side_bank[0])
                 store(group_now - 2)
@@ -486,8 +487,7 @@ def tile_localselfattention_pa_kernel(tc, q, k_scaled, hidden_states, Wv, out):
         group_e(last - 4, nc.vector.tensor_copy)
         exponentials(last - 1)
         exponentials(last)
-        invert_sums(group - 1)
-        invert_sums(group)
+        invert_sums(group // 2)
         attend(group - 2, side_bank[0])
         flip(last - 3)
         flip(last - 2)

from contextlib import ExitStack

import concourse.mybir as mybir
from concourse.masks import make_identity

F32 = mybir.dt.float32
BF16 = mybir.dt.bfloat16
U32 = mybir.dt.uint32
U8 = mybir.dt.uint8
FP8X4 = mybir.dt.float8_e4m3fn_x4
ACT = mybir.ActivationFunctionType
ALU = mybir.AluOpType

P = 128
S, HID, H, D, CHUNK = 2048, 1024, 8, 128, 512
MASK_VALUE = -1e9
K_PASS = 4 * P
N_CHUNKS = S // CHUNK
QT = CHUNK // P
N_GROUPS = N_CHUNKS * H
N_BLOCKS = N_GROUPS * QT
HID_PASSES = HID // K_PASS

QK_AHEAD = 5
CATCH_UP = (25, 27)
BLOCK_ORDER = (0, 3, 1, 2)

FLOPS = 2 * S * HID * H * D + 2 * (2 * H * D * CHUNK * (CHUNK + (N_CHUNKS - 1) * 2 * CHUNK))


def place(block):
    group, n = divmod(block, QT)
    chunk, head = divmod(group, H)
    return group, chunk, head, BLOCK_ORDER[n]


def hs_job(step):
    if -2 <= step < 2:
        return 0, step + 2
    group, half = divmod(step, 2)
    chunk, row_set = divmod(group + 3, H)
    if half == 0 and 1 <= chunk < N_CHUNKS and row_set < 4:
        return chunk, row_set
    return None


def v_job(step):
    group, half = divmod(step, 2)
    if half == 1:
        return group - 1 + sum(1 for g in CATCH_UP if g <= group)
    if group in CATCH_UP:
        return group - 1 + sum(1 for g in CATCH_UP if g < group)
    return -1


def tile_localselfattention_pa_kernel(tc, q, k_scaled, hidden_states, Wv, out):
    nc = tc.nc
    q_rows = q.flatten_outer_dims()
    k_rows = k_scaled.flatten_outer_dims()
    hs_rows = hidden_states.flatten_outer_dims()
    out_rows = out.flatten_outer_dims()

    with ExitStack() as stack:
        stack.enter_context(tc.manual_schedule())

        def ring(name, depth):
            return stack.enter_context(tc.tile_pool(name=name, bufs=depth))

        fixed = ring("fixed", 1)
        banks = stack.enter_context(tc.psum_pool(name="banks", bufs=1))

        score_bank = [banks.tile([P, CHUNK], F32, name="score_bank%d" % n) for n in range(4)]
        flip_bank = [banks.tile([P, 4 * P], F32, name="flip_bank%d" % n) for n in range(2)]
        side_bank = [banks.tile([P, 4 * P], F32, name="side_bank%d" % n) for n in range(2)]

        def pieces(bank):
            return bank[:].rearrange("p (j r) -> p j r", r=P)


        ident_f = fixed.tile([P, P], F32, name="ident_f")
        ident_b = fixed.tile([P, P], BF16, name="ident_b")
        mask_f = fixed.tile([P, P], F32, name="mask_f")
        mask_b = fixed.tile([P, P], BF16, name="mask_b")
        e_rows = [fixed.tile([P, 2 * CHUNK], BF16, name="e_rows%d" % t) for t in range(QT)]

        wv_in = fixed.tile([P, HID_PASSES, 4, H * D], BF16, name="wv_in")
        wv_codes = fixed.tile([P, H * HID_PASSES * D], U32, name="wv_codes", align_bytes=64)
        wv_scales = fixed.tile([P, H * HID_PASSES * D], U8, name="wv_scales", align_bytes=64)
        v_codes = [fixed.tile([P, H * D], U32, name="v_codes%d" % c, align_bytes=64) for c in range(N_CHUNKS)]
        v_scales = [fixed.tile([P, H * D], U8, name="v_scales%d" % c, align_bytes=64) for c in range(N_CHUNKS)]

        qk_in_ring = ring("qk_in", QK_AHEAD)
        qk_t_ring = ring("qk_t", H + 2)
        hs_in_ring = ring("hs_in", 2)
        hs_grouped_ring = ring("hs_grouped", 2)
        hs_mx_ring = ring("hs_mx", 2)
        wv_grouped_ring = ring("wv_grouped", 2)
        v_grouped_ring = ring("v_grouped", 2)
        lifted_ring = ring("lifted", 6)
        sum_ring = ring("sum", 3)
        inverse_ring = ring("inverse", 4)
        e_grouped_ring = ring("e_grouped", 7)
        e_mx_ring = ring("e_mx", 3 * QT)
        out_ring = ring("out", 26)

        qk_in, qk_t, hs_in, hs_grouped, hs_codes, hs_scales = {}, {}, {}, {}, {}, {}
        wv_grouped, v_grouped, lifted, neg_own, neg_top, row_sum, inverse = {}, {}, {}, {}, {}, {}, {}
        e_grouped, e_codes, e_scales, out_sb = {}, {}, {}, {}

        def load_qk(group):
            if not 0 <= group < N_GROUPS:
                return
            chunk, head = divmod(group, H)
            rows = slice(head * S + chunk * CHUNK, head * S + (chunk + 1) * CHUNK)
            qk_in[group] = qk_in_ring.tile([P, 2, QT, D], BF16, name="qk_in")
            nc.sync.dma_start(out=qk_in[group][:, 0], in_=q_rows[rows, :].rearrange("(t p) d -> p t d", p=P))
            nc.sync.dma_start(out=qk_in[group][:, 1], in_=k_rows[rows, :].rearrange("(t p) d -> p t d", p=P))

        def load_hs(chunk, row_set):
            if not 0 <= chunk < N_CHUNKS:
                return
            if row_set == 0:
                hs_in[chunk] = hs_in_ring.tile([P, 4, HID], BF16, name="hs_in")
            by_set = hs_rows[chunk * CHUNK : (chunk + 1) * CHUNK, :].rearrange("(u p e) k -> p u e k", p=P, e=2)
            nc.sync.dma_start(out=hs_in[chunk][:, row_set, :], in_=by_set[:, row_set // 2, row_set % 2, :])

        def load_wv(half):
            if not 0 <= half < 2:
                return
            cols = slice(half * (H * D // 2), (half + 1) * (H * D // 2))
            for g in range(HID_PASSES):
                for u in range(2):
                    first = g * K_PASS + u * 2 * P
                    nc.sync.dma_start(
                        out=wv_in[:, g, 2 * u : 2 * u + 2, cols],
                        in_=Wv[first : first + 2 * P, cols].rearrange("(p e) c -> p e c", e=2),
                    )

        def store(group):
            if not 0 <= group < N_GROUPS:
                return
            chunk, head = divmod(group, H)
            nc.sync.dma_start(
                out=out_rows[chunk * CHUNK : (chunk + 1) * CHUNK, head * D : (head + 1) * D].rearrange(
                    "(t p) d -> p t d", p=P
                ),
                in_=out_sb[group][:],
            )

        def transpose_qk(group, bank):
            if not 0 <= group < N_GROUPS:
                return
            for a in range(2):
                for t in range(QT):
                    n = a * QT + t
                    nc.tensor.transpose(
                        out=bank[:].bitcast(BF16)[:, n * P : (n + 1) * P], in_=qk_in[group][:, a, t, :], identity=ident_b[:]
                    )

        def keep_qk(group, bank, copy):
            if not 0 <= group < N_GROUPS:
                return
            qk_t[group] = qk_t_ring.tile([P, 2, CHUNK], BF16, name="qk_t")
            copy(out=qk_t[group][:], in_=bank[:].bitcast(BF16).rearrange("p (a s) -> p a s", a=2))

        def transpose_hs(job, bank):
            if job is None:
                return
            chunk, row_set = job
            words = hs_in[chunk][:, row_set, :].bitcast(F32)
            for j in range(4):
                nc.tensor.transpose(out=pieces(bank)[:, j, :], in_=words[:, j * P : (j + 1) * P], identity=ident_f[:])

        def group_hs(job, bank):
            if job is None:
                return
            hs_grouped[job] = hs_grouped_ring.tile([P, HID_PASSES * K_PASS], BF16, name="hs_grouped", align_bytes=64)
            nc.scalar.copy(
                out=hs_grouped[job][:].bitcast(F32).rearrange("p (g r u) -> p g r u", r=P, u=2),
                in_=pieces(bank).rearrange("p (g u) r -> p g r u", u=2),
            )

        def quantise_hs(job):
            if job is None:
                return
            chunk, row_set = job
            if row_set == 0:
                hs_codes[chunk] = hs_mx_ring.tile([P, 4 * HID_PASSES * P], U32, name="hs_codes", align_bytes=64)
                hs_scales[chunk] = hs_mx_ring.tile([P, 4 * HID_PASSES * P], U8, name="hs_scales", align_bytes=64)
            cols = slice(row_set * HID_PASSES * P, (row_set + 1) * HID_PASSES * P)
            nc.vector.quantize_mx(
                out=hs_codes[chunk][:, cols].bitcast(FP8X4), scales=hs_scales[chunk][:, cols], in_=hs_grouped[job][:]
            )

        def group_wv(head):
            if not 0 <= head < H:
                return
            wv_grouped[head] = wv_grouped_ring.tile([P, HID_PASSES, D, 4], BF16, name="wv_grouped", align_bytes=64)
            for g in range(HID_PASSES):
                nc.gpsimd.tensor_scalar(
                    out=wv_grouped[head][:, g],
                    in0=wv_in[:, g, :, head * D : (head + 1) * D].rearrange("p t c -> p c t"),
                    scalar1=1.0, scalar2=0.0, op0=ALU.mult, op1=ALU.add,
                )

        def quantise_wv(head):
            if not 0 <= head < H:
                return
            cols = slice(head * HID_PASSES * D, (head + 1) * HID_PASSES * D)
            nc.vector.quantize_mx(
                out=wv_codes[:, cols].bitcast(FP8X4),
                scales=wv_scales[:, cols],
                in_=wv_grouped[head][:].rearrange("p g c t -> p (g c t)"),
            )

        def project_v(group):
            if not 0 <= group < N_GROUPS:
                return
            chunk, head = divmod(group, H)
            for row_set in range(4):
                for g in range(HID_PASSES):
                    hs_cols = slice((row_set * HID_PASSES + g) * P, (row_set * HID_PASSES + g + 1) * P)
                    wv_cols = slice((head * HID_PASSES + g) * D, (head * HID_PASSES + g + 1) * D)
                    nc.tensor.matmul_mx(
                        out=pieces(side_bank[1])[:, row_set, :],
                        lhsT=hs_codes[chunk][:, hs_cols].bitcast(FP8X4),
                        lhsT_scale=hs_scales[chunk][:, hs_cols],
                        rhs=wv_codes[:, wv_cols].bitcast(FP8X4),
                        rhs_scale=wv_scales[:, wv_cols],
                        start=(g == 0),
                        stop=(g == HID_PASSES - 1),
                    )

        def round_v(group, copy):
            if not 0 <= group < N_GROUPS:
                return
            v_grouped[group] = v_grouped_ring.tile([P, D, 4], BF16, name="v_grouped", align_bytes=64)
            copy(out=v_grouped[group][:], in_=pieces(side_bank[1]).rearrange("p t d -> p d t"))

        def quantise_v(group):
            if not 0 <= group < N_GROUPS:
                return
            chunk, head = divmod(group, H)
            cols = slice(head * D, (head + 1) * D)
            nc.vector.quantize_mx(
                out=v_codes[chunk][:, cols].bitcast(FP8X4),
                scales=v_scales[chunk][:, cols],
                in_=v_grouped[group][:].rearrange("p d t -> p (d t)"),
            )

        def scores(block):
            if not 0 <= block < N_BLOCKS:
                return
            group, chunk, head, t = place(block)
            queries = qk_t[group][:, 0, t * P : (t + 1) * P]
            back, own = score_bank[2 * (block % 2)], score_bank[2 * (block % 2) + 1]
            width = (t + 1) * P
            nc.tensor.matmul(out=own[:, 0:width], lhsT=queries, rhs=qk_t[group][:, 1, 0:width], start=True, stop=False)
            nc.tensor.matmul(out=own[:, t * P : width], lhsT=ident_b[:], rhs=mask_b[:], start=False, stop=True)
            if chunk > 0:
                nc.tensor.matmul(out=back[:], lhsT=queries, rhs=qk_t[group - H][:, 1, :], start=True, stop=True)

        def lift_own(block):
            if not 0 <= block < N_BLOCKS:
                return
            group, chunk, head, t = place(block)
            lifted[block] = lifted_ring.tile([P, 2 * CHUNK], F32, name="lifted")
            neg_own[block] = lifted_ring.tile([P, 1], F32, name="neg_own")
            width = (t + 1) * P
            nc.vector.tensor_scalar(
                out=lifted[block][:, CHUNK : CHUNK + width], in0=score_bank[2 * (block % 2) + 1][:, 0:width],
                scalar1=-1.0, scalar2=None, op0=ALU.mult, op1=ALU.min, accum_out=neg_own[block][:],
            )

        def lift_back(block):
            if not 0 <= block < N_BLOCKS:
                return
            if block < H * QT:
                neg_top[block] = neg_own[block]
                return
            neg_top[block] = lifted_ring.tile([P, 1], F32, name="neg_top")
            nc.vector.tensor_scalar(
                out=lifted[block][:, 0:CHUNK], in0=score_bank[2 * (block % 2)][:], scalar1=-1.0,
                scalar2=neg_own[block][:], op0=ALU.mult, op1=ALU.min, accum_out=neg_top[block][:],
            )

        def exponentials(block):
            if not 0 <= block < N_BLOCKS:
                return
            group, chunk, head, t = place(block)
            if block % (2 * QT) == 0:
                row_sum[group // 2] = sum_ring.tile([P, 2 * QT], F32, name="row_sum")
            keys = slice(0 if chunk > 0 else CHUNK, CHUNK + (t + 1) * P)
            column = group % 2 * QT + t
            nc.scalar.activation(
                out=e_rows[t][:, keys], in_=lifted[block][:, keys], func=ACT.Exp,
                bias=neg_top[block][:], scale=-1.0, accum_out=row_sum[group // 2][:, column : column + 1],
            )

        def invert_sums(group_pair):
            if not 0 <= group_pair < N_GROUPS // 2:
                return
            inverse[group_pair] = inverse_ring.tile([P, 2 * QT], F32, name="inverse")
            nc.vector.reciprocal(out=inverse[group_pair][:], in_=row_sum[group_pair][:])

        def first_pass(chunk):
            return 0 if chunk > 0 else 1

        def flip_to(block):
            return flip_bank[block % 2] if block < N_BLOCKS - 2 else score_bank[block % 2]

        def flip(block):
            if not 0 <= block < N_BLOCKS:
                return
            group, chunk, head, t = place(block)
            words = e_rows[t][:].bitcast(F32)
            last = 3 if t < 2 and 0 < block < N_BLOCKS - 2 else 4
            for j in range(2 * first_pass(chunk), last):
                nc.tensor.transpose(
                    out=pieces(flip_to(block))[:, j, :], in_=words[:, j * P : (j + 1) * P], identity=ident_f[:]
                )

        def group_e(block, copy):
            if not 0 <= block < N_BLOCKS:
                return
            group, chunk, head, t = place(block)
            g0 = first_pass(chunk)
            e_grouped[block] = e_grouped_ring.tile([P, 2 * K_PASS], BF16, name="e_grouped", align_bytes=64)
            copy(
                out=e_grouped[block][:].bitcast(F32)[:, g0 * 2 * P : 4 * P].rearrange("p (g r u) -> p g r u", r=P, u=2),
                in_=pieces(flip_to(block))[:, 2 * g0 : 4, :].rearrange("p (g u) r -> p g r u", u=2),
            )

        def quantise_e(block):
            if not 0 <= block < N_BLOCKS:
                return
            group, chunk, head, t = place(block)
            g0 = first_pass(chunk)
            e_codes[block] = e_mx_ring.tile([P, 2 * P], U32, name="e_codes", align_bytes=64)
            e_scales[block] = e_mx_ring.tile([P, 2 * P], U8, name="e_scales", align_bytes=64)
            nc.vector.quantize_mx(
                out=e_codes[block][:, g0 * P : 2 * P].bitcast(FP8X4),
                scales=e_scales[block][:, g0 * P : 2 * P],
                in_=e_grouped[block][:, g0 * K_PASS : 2 * K_PASS],
            )

        def attend(group, bank, part=range(QT)):
            if not 0 <= group < N_GROUPS:
                return
            chunk, head = divmod(group, H)
            for n in part:
                t = BLOCK_ORDER[n]
                block = group * QT + n
                for g in range(first_pass(chunk), 2):
                    nc.tensor.matmul_mx(
                        out=pieces(bank)[:, t, :],
                        lhsT=e_codes[block][:, g * P : (g + 1) * P].bitcast(FP8X4),
                        lhsT_scale=e_scales[block][:, g * P : (g + 1) * P],
                        rhs=v_codes[chunk - 1 + g][:, head * D : (head + 1) * D].bitcast(FP8X4),
                        rhs_scale=v_scales[chunk - 1 + g][:, head * D : (head + 1) * D],
                        start=(g == first_pass(chunk)),
                        stop=(g == 1),
                    )

        def normalise(group, bank, first=0, end=QT):
            if not 0 <= group < N_GROUPS:
                return
            if group not in out_sb:
                out_sb[group] = out_ring.tile([P, QT, D], F32, name="out_sb")
            nc.vector.tensor_tensor(
                out=out_sb[group][:, first:end, :], in0=pieces(bank)[:, first:end, :],
                in1=inverse[group // 2][:, group % 2 * QT + first : group % 2 * QT + end].unsqueeze(2).to_broadcast([P, end - first, D]), op=ALU.mult,
            )

        def normalise_on_scalar(group, bank, tiles=range(QT)):
            if group not in out_sb:
                out_sb[group] = out_ring.tile([P, QT, D], F32, name="out_sb")
            for t in tiles:
                nc.scalar.activation(
                    out=out_sb[group][:, t, :], in_=pieces(bank)[:, t, :], func=ACT.Copy, scale=inverse[group // 2][:, group % 2 * QT + t : group % 2 * QT + t + 1]
                )

        load_qk(0)
        load_qk(1)
        load_hs(0, 0)
        load_hs(0, 1)
        load_qk(2)
        load_hs(0, 2)
        load_hs(0, 3)
        load_wv(0)
        load_qk(3)
        load_wv(1)
        load_qk(4)

        make_identity(nc, ident_f[:])
        make_identity(nc, ident_b[:])
        nc.gpsimd.memset(mask_f[:], 0.0)
        nc.gpsimd.affine_select(
            out=mask_f[:], in_=mask_f[:], compare_op=ALU.is_ge, fill=MASK_VALUE, base=0, pattern=[[-1, P]],
            channel_multiplier=1,
        )
        nc.vector.tensor_copy(out=mask_b[:], in_=mask_f[:])
        for t in range(QT - 1):
            nc.vector.memset(e_rows[t][:, CHUNK + (t + 1) * P : 2 * CHUNK], 0.0)

        def qk_bank(group):
            return score_bank[0] if group < H else side_bank[0]

        transpose_qk(0, side_bank[0])
        keep_qk(0, side_bank[0], nc.scalar.copy)
        transpose_qk(1, side_bank[1])
        keep_qk(1, side_bank[1], nc.vector.tensor_copy)
        for block in range(2):
            scores(block)
        for block in range(2):
            lift_own(block)
            lift_back(block)
        transpose_hs(hs_job(-2), side_bank[0])
        for block in range(2, 4):
            scores(block)
        transpose_hs(hs_job(-1), side_bank[1])

        for step in range(2 * N_GROUPS - 1):
            group_now, half = divmod(step, 2)
            pair = 2 * step
            lift_own(pair + 2)
            quantise_e(pair - 6)
            lift_back(pair + 2)
            if (v_job(step - 1) % 2 == 0 and v_job(step - 1) >= H):
                round_v(v_job(step - 1), nc.vector.tensor_copy)
            lift_own(pair + 3)
            quantise_e(pair - 5)
            lift_back(pair + 3)
            group_e(pair - 4, nc.scalar.copy)
            group_e(pair - 3, nc.scalar.copy)
            if half == 1:
                keep_qk(group_now + 2, qk_bank(group_now + 2), nc.scalar.copy)
            if step > 2:
                group_hs(hs_job(step - 1), side_bank[1])
            exponentials(pair)
            exponentials(pair + 1)
            if (v_job(step - 1) % 2 == 1 or v_job(step - 1) < H):
                round_v(v_job(step - 1), nc.scalar.copy)
            if step == 0:
                group_hs(hs_job(-2), side_bank[0])
                quantise_hs(hs_job(-2))
            if step <= 2:
                group_hs(hs_job(step - 1), side_bank[1])
            if half == 0:
                flip(pair - 2)
                flip(pair - 1)
                transpose_qk(group_now + 2, qk_bank(group_now + 2))
                scores(pair + 4)
                transpose_hs(hs_job(step), side_bank[1])
                project_v(v_job(step))
                scores(pair + 5)
            else:
                flip(pair - 2)
                flip(pair - 1)
                attend(group_now - 2, side_bank[0])
                scores(pair + 4)
                transpose_hs(hs_job(step), side_bank[1])
                project_v(v_job(step))
                scores(pair + 5)
            if half == 1:
                group_wv(group_now)
            if half == 0:
                load_qk(group_now + QK_AHEAD)
                if group_now % H == 0:
                    for row_set in range(4):
                        load_hs(group_now // H + 1, row_set)
            quantise_hs(hs_job(step - 1))
            if half == 0:
                quantise_wv(group_now - 1)
            if half == 0 and group_now % 2 == 0:
                invert_sums(group_now // 2 - 1)
            if half == 1:
                normalise(group_now - 2, side_bank[0])
                store(group_now - 2)
            quantise_v(v_job(step - 1))

        last = N_BLOCKS - 1
        group = N_GROUPS - 1
        quantise_e(last - 7)
        quantise_e(last - 6)
        group_e(last - 5, nc.scalar.copy)
        group_e(last - 4, nc.vector.tensor_copy)
        exponentials(last - 1)
        exponentials(last)
        invert_sums(group // 2)
        attend(group - 2, side_bank[0])
        flip(last - 3)
        flip(last - 2)
        quantise_e(last - 5)
        quantise_e(last - 4)
        group_e(last - 3, nc.scalar.copy)
        group_e(last - 2, nc.vector.tensor_copy)
        flip(last - 1)
        flip(last)
        attend(group - 1, side_bank[1])
        quantise_e(last - 3)
        quantise_e(last - 2)
        group_e(last - 1, nc.scalar.copy)
        group_e(last, nc.vector.tensor_copy)
        attend(group, score_bank[2], (0, 1))
        normalise_on_scalar(group - 2, side_bank[0])
        store(group - 2)
        normalise_on_scalar(group - 1, side_bank[1])
        store(group - 1)
        quantise_e(last - 1)
        quantise_e(last)
        attend(group, score_bank[3], (2, 3))
        normalise_on_scalar(group, score_bank[2], (0, 3))
        normalise(group, score_bank[3], 1, 3)
        store(group)
